import numpy as np
import ml_dtypes


def mxq(x, axis, fmt="e4m3"):
    dtype, down = {"e4m3": (ml_dtypes.float8_e4m3fn, 7), "e5m2": (ml_dtypes.float8_e5m2, 14)}[fmt]
    v = np.moveaxis(np.asarray(x, np.float32).astype(ml_dtypes.bfloat16).astype(np.float64), axis, -1)
    blocks = v.reshape(v.shape[:-1] + (-1, 32))
    amax = np.abs(blocks).max(-1, keepdims=True)
    byte = np.maximum(np.where(amax > 0, np.frexp(amax)[1] - 1 + 127, 0) - down, 1)
    scale = np.exp2(byte - 127.0)
    codes = (blocks / scale).astype(np.float32).astype(dtype).astype(np.float64)
    return np.moveaxis((codes * scale).reshape(v.shape), -1, axis)


WIDE = False


def mx_kscale(k):
    if not WIDE:
        return np.ones(k)
    levels = np.array([20, -20, 10, -10, 0])
    a = np.random.permutation(np.resize(levels, k // 512 * 4)).reshape(k // 512, 4)
    idx = np.arange(k)
    return np.exp2(a[idx // 512, idx % 128 // 32])


BF16 = ml_dtypes.bfloat16


def bf(x):
    return np.asarray(x, np.float32).astype(BF16)


def f64(x):
    return np.asarray(x).astype(np.float64)


B, C, H, W, KS, CO = 8, 32, 35, 35, 4, 1024
OH, OW = H - KS + 1, W - KS + 1
Q = C * KS * KS


def unfold_patches(x, k):
    oh, ow = x.shape[2] - k + 1, x.shape[3] - k + 1
    rows = []
    for di in range(k):
        cols = [x[:, :, di:di + oh, dj:dj + ow] for dj in range(k)]
        rows.append(np.stack(cols, axis=-1))
    return np.stack(rows, axis=-2)


def setup_inputs():
    u = mx_kscale(CO)
    x = np.random.standard_normal((B, C, H, W))
    weights = np.random.standard_normal((Q, CO)) / np.sqrt(Q) / u[None, :]
    bias = np.random.standard_normal(CO) * 0.3
    g = np.random.standard_normal((B, CO, OH, OW)) * np.exp2(np.random.randint(-12, 1, (B, 1, OH, OW))) * u[None, :, None, None]
    return {"x": bf(x), "weights": bf(weights), "bias": bf(bias), "grad_out": bf(g)}


def reference(x, weights, bias, grad_out):
    g = np.transpose(f64(grad_out), (0, 2, 3, 1))
    d = mxq(g, 3, "e5m2") @ mxq(f64(weights), 1, "e4m3").T
    e = d.reshape(B, C, OH, OW, KS, KS)
    dx = np.zeros((B, C, H, W))
    for di in range(KS):
        for dj in range(KS):
            dx[:, :, di:di + OH, dj:dj + OW] += e[:, :, :, :, di, dj]
    return dx

@@ -1,0 +1,282 @@
+from contextlib import ExitStack
+
+import concourse.mybir as mybir
+from concourse.masks import make_identity
+
+FLOPS = 2 * 8192 * 1024 * 512
+BYTES = 8 * 1024 * 1024 * 2 + 512 * 1024 * 2 + 8 * 32 * 35 * 35 * 4
+
+BF16 = mybir.dt.bfloat16
+F32 = mybir.dt.float32
+I32 = mybir.dt.int32
+U32 = mybir.dt.uint32
+U8 = mybir.dt.uint8
+E4X4 = mybir.dt.float8_e4m3fn_x4
+E5X4 = mybir.dt.float8_e5m2_x4
+
+P = 128
+PAIRS = 4
+KP = 2
+ROWS = 35
+RC = 64
+NIN = 147
+NWIN = 18
+ZT = 18
+UNITS = 16
+GROUPS = 8
+AHEAD = 3
+
+
+def tile_conv2d_t_kernel(tc, x, weights, bias, grad_out, out):
+    nc = tc.nc
+    with ExitStack() as ctx:
+        ctx.enter_context(tc.manual_schedule())
+        keep = ctx.enter_context(tc.tile_pool(name="keep", bufs=1))
+        rawp = ctx.enter_context(tc.tile_pool(name="rawp", bufs=2 * AHEAD))
+        grpp = ctx.enter_context(tc.tile_pool(name="grpp", bufs=4))
+        outp = ctx.enter_context(tc.tile_pool(name="outp", bufs=4))
+        accp = ctx.enter_context(tc.psum_pool(name="accp", bufs=6))
+        finp = ctx.enter_context(tc.psum_pool(name="finp", bufs=2))
+
+        codes = keep.tile([P, KP, NIN * RC], U32, align_bytes=64)
+        scl = keep.tile([P, KP, NIN * RC], U8, align_bytes=64)
+        wc = keep.tile([P, KP * 512], U32, align_bytes=64)
+        ws = keep.tile([P, KP * 512], U8, align_bytes=64)
+        wraw = keep.tile([P, 4, 1024], BF16)
+        wg = keep.tile([P, 4096], BF16, align_bytes=64)
+        ident = keep.tile([P, P], F32)
+        cmat = keep.tile([P, ROWS], F32)
+        racc_a = keep.tile([P, ZT * P], F32)
+        racc_b = keep.tile([P, ZT * P], F32)
+        raccs = [racc_a, racc_b]
+        out2 = out.rearrange("b c h w -> (b c) (h w)")
+
+        raws = {}
+
+        def load_w(kp):
+            wsrc = weights.rearrange("(j di dj) k -> dj j di k", di=4, dj=4)
+            for dj in range(4):
+                nc.sync.dma_start(
+                    out=wraw[dj:P:4, :, kp * 512 : (kp + 1) * 512],
+                    in_=wsrc[dj][:, :, kp * 512 : (kp + 1) * 512],
+                )
+
+        def load_group(grp):
+            pi, kp = divmod(grp, KP)
+            for be in range(2):
+                raw = rawp.tile([P, 4096], BF16, tag="raw", name="raw%d_%d" % (grp, be))
+                nc.sync.dma_start(
+                    out=raw[:],
+                    in_=grad_out[2 * pi + be, kp * 512 : (kp + 1) * 512].rearrange("(p j) u v -> p (j u v)", j=4),
+                )
+                raws[(grp, be)] = raw
+
+        wts = {}
+        w32 = wraw[:].rearrange("p di k -> p (di k)").bitcast(F32)
+        wg32 = wg[:].bitcast(F32).rearrange("p (kp di m e) -> p kp di m e", kp=2, di=4, e=2)
+
+        def w_transposes(kp):
+            for dp in range(2):
+                wt = accp.tile([P, 4, P], F32, tag="acc", name="wt%d_%d" % (kp, dp))
+                for d in range(2):
+                    for e in range(2):
+                        s = (2 * dp + d) * 512 + kp * 256 + e
+                        nc.tensor.transpose(wt[:, 2 * d + e, :], w32[:, s : s + 255 : 2], ident[:])
+                wts[(kp, dp)] = wt
+
+        def w_copies(kp):
+            for dp in range(2):
+                src = wts[(kp, dp)][:].rearrange("p (d e) m -> p d m e", e=2)
+                dst = wg32[:, kp, 2 * dp : 2 * dp + 2, :, :]
+                if dp == 0:
+                    nc.vector.tensor_copy(out=dst, in_=src)
+                else:
+                    nc.scalar.copy(out=dst, in_=src)
+
+        def w_quantise(kp):
+            nc.vector.quantize_mx(
+                out=wc[:, kp * 512 : (kp + 1) * 512].bitcast(E4X4),
+                scales=ws[:, kp * 512 : (kp + 1) * 512],
+                in_=wg[:, kp * 2048 : (kp + 1) * 2048],
+            )
+
+        ggs = {}
+
+        def regroup(s):
+            grp, half = divmod(s, 2)
+            kp = grp % KP
+            gg = grpp.tile([P, 4096], BF16, tag="grp", align_bytes=64, name="gg%d" % s)
+            ggs[s] = gg
+            g6 = gg[:].rearrange("p (a f b c j) -> p b a c j f", a=4, f=4, b=2, c=32, j=4)
+            r5 = [
+                raws[(grp, be)][:].rearrange("p (j c a f) -> p a c j f", j=4, c=32, a=8, f=4)
+                for be in range(2)
+            ]
+            a0 = 4 * half
+            nc.vector.tensor_copy(out=g6[:, 0], in_=r5[0][:, a0 : a0 + 4])
+            first = 0
+            if kp == 0:
+                nc.vector.tensor_copy(out=g6[:, 1, 0:2], in_=r5[1][:, a0 : a0 + 2])
+                first = 2
+            for a in range(first, 4):
+                nc.scalar.copy(out=g6[:, 1, a], in_=r5[1][:, a0 + a])
+
+        def quantise(s):
+            grp, half = divmod(s, 2)
+            pi, kp = divmod(grp, KP)
+            c0 = (ROWS * pi + 3 + 16 * half) * RC
+            parts = 2 if s == 0 else 1
+            wid = 1024 // parts
+            for q in range(parts):
+                nc.vector.quantize_mx(
+                    out=codes[:, kp, c0 + q * wid : c0 + (q + 1) * wid].bitcast(E5X4),
+                    scales=scl[:, kp, c0 + q * wid : c0 + (q + 1) * wid],
+                    in_=ggs[s][:, 4 * q * wid : 4 * (q + 1) * wid],
+                )
+
+        accs = {}
+        npass = {}
+        nextwin = [0, 0]
+        fins = {}
+        otiles = {}
+        state = {"zdone": 0, "rows": 0, "loads": AHEAD, "e2": 0, "st": 0}
+        pending_e2 = []
+        pending_st = []
+
+        def final_upto(rows_done):
+            while state["zdone"] < PAIRS * ZT:
+                pi, z = divmod(state["zdone"], ZT)
+                blk, zz = divmod(z, 9)
+                need = ROWS * pi + min(18 * blk + 9 + zz, ROWS - 1)
+                if need >= rows_done:
+                    break
+                if zz == 0:
+                    fins[(pi, blk)] = finp.tile([P, 9, ROWS], F32, tag="fin", name="fin%d_%d" % (pi, blk))
+                nc.tensor.matmul(
+                    out=fins[(pi, blk)][:, zz, :],
+                    lhsT=raccs[pi % 2][:, z * P : (z + 1) * P],
+                    rhs=cmat[:],
+                    start=True,
+                    stop=True,
+                )
+                if zz == 8:
+                    pending_e2.append((pi, blk))
+                state["zdone"] += 1
+
+        def flush_st():
+            if state["loads"] < GROUPS:
+                return
+            for pi, blk in pending_st[state["st"] :]:
+                for y2 in range(2):
+                    n = 315 if 18 * blk + 9 * y2 + 9 <= ROWS else 280
+                    col = (18 * blk + 9 * y2) * ROWS
+                    nc.sync.dma_start(
+                        out=out2[64 * pi : 64 * pi + 64, col : col + n],
+                        in_=otiles[pi][64 * y2 : 64 * y2 + 64, 315 * blk : 315 * blk + n],
+                    )
+            state["st"] = len(pending_st)
+
+        def flush_e2():
+            for pi, blk in pending_e2[state["e2"] :]:
+                if blk == 0:
+                    otiles[pi] = outp.tile([P, ZT * ROWS], F32, tag="o", name="o%d" % pi)
+                nc.scalar.copy(
+                    out=otiles[pi][:, 315 * blk : 315 * blk + 315],
+                    in_=fins[(pi, blk)][:].rearrange("p z w -> p (z w)"),
+                )
+                pending_st.append((pi, blk))
+            state["e2"] = len(pending_e2)
+            flush_st()
+
+        def evacuate(om):
+            r = 0
+            while r < 8 and 8 * om + r < PAIRS * ROWS:
+                pi, h = divmod(8 * om + r, ROWS)
+                n = min(8 - r, 9 - h % 9, ROWS - h)
+                blk, hh = divmod(h, 18)
+                y2, zz = divmod(hh, 9)
+                z0 = 9 * blk + zz
+                dst = raccs[pi % 2][:].rearrange("p (z y c) -> p z y c", y=2, c=RC)
+                nc.scalar.copy(
+                    out=dst[:, z0 : z0 + n, y2, :],
+                    in_=accs[om][:, r * RC : (r + n) * RC].rearrange("p (r c) -> p r c", c=RC),
+                )
+                r += n
+
+        def multiply(s):
+            grp, half = divmod(s, 2)
+            pi, kp = divmod(grp, KP)
+            if half == 0:
+                avail = ROWS * pi + 3 + 16
+            elif pi < PAIRS - 1:
+                avail = ROWS * (pi + 1) + 3
+            else:
+                avail = NIN
+            while nextwin[kp] < NWIN and 8 * nextwin[kp] + 10 < avail:
+                om = nextwin[kp]
+                if om not in accs:
+                    accs[om] = accp.tile([P, 512], F32, tag="acc", name="acc%d" % om)
+                    npass[om] = 0
+                for di in range(4):
+                    c0 = (8 * om + 3 - di) * RC
+                    o = kp * 512 + di * P
+                    nc.tensor.matmul_mx(
+                        out=accs[om][:],
+                        lhsT=wc[:, o : o + P].bitcast(E4X4),
+                        lhsT_scale=ws[:, o : o + P],
+                        rhs=codes[:, kp, c0 : c0 + 512].bitcast(E5X4),
+                        rhs_scale=scl[:, kp, c0 : c0 + 512],
+                        start=(npass[om] == 0),
+                        stop=(npass[om] == 7),
+                    )
+                    npass[om] += 1
+                if npass[om] == 8:
+                    evacuate(om)
+                    final_upto(state["rows"])
+                    state["rows"] = 8 * om + 8
+                nextwin[kp] += 1
+
+        load_w(0)
+        load_group(0)
+        load_w(1)
+        load_group(1)
+        load_group(2)
+        make_identity(nc, ident[:])
+        for pi in range(PAIRS + 1):
+            g0 = ROWS * pi
+            g1 = g0 + 3 if pi < PAIRS else NIN
+            nc.vector.memset(codes[:, :, g0 * RC : g1 * RC].bitcast(I32), 0)
+            nc.vector.memset(scl[:, :, g0 * RC : g1 * RC].bitcast(I32), 0)
+        for racc in raccs:
+            nc.vector.memset(racc[:, (ZT - 1) * P + RC : ZT * P], 0.0)
+        nc.vector.memset(cmat[:], 0.0)
+        for dj in range(4):
+            nc.vector.tensor_tensor(
+                out=cmat[:, dj : dj + 32],
+                in0=cmat[:, dj : dj + 32],
+                in1=ident[:, dj:P:4],
+                op=mybir.AluOpType.add,
+            )
+        w_transposes(0)
+        w_copies(0)
+        w_quantise(0)
+        regroup(0)
+        for n in range(UNITS + 1):
+            flush_e2()
+            if n == 2:
+                w_copies(1)
+            if n + 1 < UNITS:
+                regroup(n + 1)
+                if n % 2 == 0 and state["loads"] < GROUPS:
+                    load_group(state["loads"])
+                    state["loads"] += 1
+            if n == 2:
+                w_quantise(1)
+            if n < UNITS:
+                quantise(n)
+            if n >= 1:
+                multiply(n - 1)
+            if n == 1:
+                w_transposes(1)
+        final_upto(PAIRS * ROWS + 4)
+        flush_e2()

@@ -25,6 +25,12 @@ ZT = 18
 UNITS = 16
 GROUPS = 8
 AHEAD = 3
+S_SLICES = (3, 3, 4, 4)
+S_SLICES_LAST = {0: 2, 14: 3, 15: 2}
+EARLY = 1
+SA = 0
+GBUFS = 4
+SPLIT_Q = (0, 15)
 
 
 def tile_conv2d_t_kernel(tc, x, weights, bias, grad_out, out):
@@ -33,7 +39,7 @@ def tile_conv2d_t_kernel(tc, x, weights, bias, grad_out, out):
         ctx.enter_context(tc.manual_schedule())
         keep = ctx.enter_context(tc.tile_pool(name="keep", bufs=1))
         rawp = ctx.enter_context(tc.tile_pool(name="rawp", bufs=2 * AHEAD))
-        grpp = ctx.enter_context(tc.tile_pool(name="grpp", bufs=4))
+        grpp = ctx.enter_context(tc.tile_pool(name="grpp", bufs=GBUFS))
         outp = ctx.enter_context(tc.tile_pool(name="outp", bufs=4))
         accp = ctx.enter_context(tc.psum_pool(name="accp", bufs=6))
         finp = ctx.enter_context(tc.psum_pool(name="finp", bufs=2))
@@ -57,7 +63,7 @@ def tile_conv2d_t_kernel(tc, x, weights, bias, grad_out, out):
             wsrc = weights.rearrange("(j di dj) k -> dj j di k", di=4, dj=4)
             for dj in range(4):
                 nc.sync.dma_start(
-                    out=wraw[dj:P:4, :, kp * 512 : (kp + 1) * 512],
+                    out=wraw[32 * dj : 32 * dj + 32, :, kp * 512 : (kp + 1) * 512],
                     in_=wsrc[dj][:, :, kp * 512 : (kp + 1) * 512],
                 )
 
@@ -102,22 +108,25 @@ def tile_conv2d_t_kernel(tc, x, weights, bias, grad_out, out):
 
         ggs = {}
 
-        def regroup(s):
+        def views(s):
             grp, half = divmod(s, 2)
-            kp = grp % KP
-            gg = grpp.tile([P, 4096], BF16, tag="grp", align_bytes=64, name="gg%d" % s)
-            ggs[s] = gg
-            g6 = gg[:].rearrange("p (a f b c j) -> p b a c j f", a=4, f=4, b=2, c=32, j=4)
+            if s not in ggs:
+                ggs[s] = grpp.tile([P, 4096], BF16, tag="grp", align_bytes=64, name="gg%d" % s)
+            g6 = ggs[s][:].rearrange("p (a f b c j) -> p b a c j f", a=4, f=4, b=2, c=32, j=4)
             r5 = [
                 raws[(grp, be)][:].rearrange("p (j c a f) -> p a c j f", j=4, c=32, a=8, f=4)
                 for be in range(2)
             ]
-            a0 = 4 * half
+            return g6, r5, 4 * half, 4 - S_SLICES_LAST.get(s, S_SLICES[s % 4])
+
+        def regroup_v(s):
+            g6, r5, a0, first = views(s)
             nc.vector.tensor_copy(out=g6[:, 0], in_=r5[0][:, a0 : a0 + 4])
-            first = 0
-            if kp == 0:
-                nc.vector.tensor_copy(out=g6[:, 1, 0:2], in_=r5[1][:, a0 : a0 + 2])
-                first = 2
+            if first > 0:
+                nc.vector.tensor_copy(out=g6[:, 1, 0:first], in_=r5[1][:, a0 : a0 + first])
+
+        def regroup_s(s):
+            g6, r5, a0, first = views(s)
             for a in range(first, 4):
                 nc.scalar.copy(out=g6[:, 1, a], in_=r5[1][:, a0 + a])
 
@@ -125,7 +134,7 @@ def tile_conv2d_t_kernel(tc, x, weights, bias, grad_out, out):
             grp, half = divmod(s, 2)
             pi, kp = divmod(grp, KP)
             c0 = (ROWS * pi + 3 + 16 * half) * RC
-            parts = 2 if s == 0 else 1
+            parts = 2 if s in SPLIT_Q else 1
             wid = 1024 // parts
             for q in range(parts):
                 nc.vector.quantize_mx(
@@ -254,25 +263,32 @@ def tile_conv2d_t_kernel(tc, x, weights, bias, grad_out, out):
             nc.vector.tensor_tensor(
                 out=cmat[:, dj : dj + 32],
                 in0=cmat[:, dj : dj + 32],
-                in1=ident[:, dj:P:4],
+                in1=ident[:, 32 * dj : 32 * dj + 32],
                 op=mybir.AluOpType.add,
             )
         w_transposes(0)
         w_copies(0)
         w_quantise(0)
-        regroup(0)
+        regroup_v(0)
+        for s in range(SA + 1):
+            regroup_s(s)
+        quantise(0)
         for n in range(UNITS + 1):
             flush_e2()
             if n == 2:
                 w_copies(1)
+            if 1 <= n < EARLY:
+                quantise(n)
+            if n + 1 + SA < UNITS:
+                regroup_s(n + 1 + SA)
             if n + 1 < UNITS:
-                regroup(n + 1)
+                regroup_v(n + 1)
                 if n % 2 == 0 and state["loads"] < GROUPS:
                     load_group(state["loads"])
                     state["loads"] += 1
             if n == 2:
                 w_quantise(1)
-            if n < UNITS:
+            if EARLY <= n < UNITS:
                 quantise(n)
             if n >= 1:
                 multiply(n - 1)

@@ -25,9 +25,10 @@ ZT = 18
 UNITS = 16
 GROUPS = 8
 AHEAD = 3
-S_SLICES = (3, 3, 4, 4)
-S_SLICES_LAST = {0: 2, 14: 3, 15: 2}
-EARLY = 1
+S_SLICES = (2, 1, 2, 2)
+S_SLICES_LAST = {0: 2, 15: 2}
+EARLY = 2
+FM_EVERY = 1
 SA = 0
 GBUFS = 4
 SPLIT_Q = (0, 15)
@@ -48,10 +49,12 @@ def tile_conv2d_t_kernel(tc, x, weights, bias, grad_out, out):
         scl = keep.tile([P, KP, NIN * RC], U8, align_bytes=64)
         wc = keep.tile([P, KP * 512], U32, align_bytes=64)
         ws = keep.tile([P, KP * 512], U8, align_bytes=64)
-        wraw = keep.tile([P, 4, 1024], BF16)
+        wraw_a = keep.tile([P, 4, 512], BF16)
+        wraw_b = keep.tile([P, 4, 512], BF16)
+        wraws = [wraw_a, wraw_b]
         wg = keep.tile([P, 4096], BF16, align_bytes=64)
         ident = keep.tile([P, P], F32)
-        cmat = keep.tile([P, ROWS], F32)
+        cmat = keep.tile([P, ROWS + 1], F32)
         racc_a = keep.tile([P, ZT * P], F32)
         racc_b = keep.tile([P, ZT * P], F32)
         raccs = [racc_a, racc_b]
@@ -63,7 +66,7 @@ def tile_conv2d_t_kernel(tc, x, weights, bias, grad_out, out):
             wsrc = weights.rearrange("(j di dj) k -> dj j di k", di=4, dj=4)
             for dj in range(4):
                 nc.sync.dma_start(
-                    out=wraw[32 * dj : 32 * dj + 32, :, kp * 512 : (kp + 1) * 512],
+                    out=wraws[kp][32 * dj : 32 * dj + 32],
                     in_=wsrc[dj][:, :, kp * 512 : (kp + 1) * 512],
                 )
 
@@ -78,15 +81,15 @@ def tile_conv2d_t_kernel(tc, x, weights, bias, grad_out, out):
                 raws[(grp, be)] = raw
 
         wts = {}
-        w32 = wraw[:].rearrange("p di k -> p (di k)").bitcast(F32)
         wg32 = wg[:].bitcast(F32).rearrange("p (kp di m e) -> p kp di m e", kp=2, di=4, e=2)
 
         def w_transposes(kp):
+            w32 = wraws[kp][:].rearrange("p di k -> p (di k)").bitcast(F32)
             for dp in range(2):
                 wt = accp.tile([P, 4, P], F32, tag="acc", name="wt%d_%d" % (kp, dp))
                 for d in range(2):
                     for e in range(2):
-                        s = (2 * dp + d) * 512 + kp * 256 + e
+                        s = (2 * dp + d) * 256 + e
                         nc.tensor.transpose(wt[:, 2 * d + e, :], w32[:, s : s + 255 : 2], ident[:])
                 wts[(kp, dp)] = wt
 
@@ -121,14 +124,14 @@ def tile_conv2d_t_kernel(tc, x, weights, bias, grad_out, out):
 
         def regroup_v(s):
             g6, r5, a0, first = views(s)
-            nc.vector.tensor_copy(out=g6[:, 0], in_=r5[0][:, a0 : a0 + 4])
-            if first > 0:
-                nc.vector.tensor_copy(out=g6[:, 1, 0:first], in_=r5[1][:, a0 : a0 + first])
+            for be in range(2):
+                nc.vector.tensor_copy(out=g6[:, be, 0:first], in_=r5[be][:, a0 : a0 + first])
 
         def regroup_s(s):
             g6, r5, a0, first = views(s)
             for a in range(first, 4):
-                nc.scalar.copy(out=g6[:, 1, a], in_=r5[1][:, a0 + a])
+                for be in range(2):
+                    nc.scalar.copy(out=g6[:, be, a], in_=r5[be][:, a0 + a])
 
         def quantise(s):
             grp, half = divmod(s, 2)
@@ -148,19 +151,21 @@ def tile_conv2d_t_kernel(tc, x, weights, bias, grad_out, out):
         nextwin = [0, 0]
         fins = {}
         otiles = {}
-        state = {"zdone": 0, "rows": 0, "loads": AHEAD, "e2": 0, "st": 0}
+        state = {"zdone": 0, "rows": 0, "loads": AHEAD, "e2": 0, "st": 0, "next_rows": 0}
         pending_e2 = []
         pending_st = []
 
-        def final_upto(rows_done):
-            while state["zdone"] < PAIRS * ZT:
+        def final_upto(rows_done, limit):
+            count = 0
+            while state["zdone"] < PAIRS * ZT and count < limit:
+                count += 1
                 pi, z = divmod(state["zdone"], ZT)
                 blk, zz = divmod(z, 9)
                 need = ROWS * pi + min(18 * blk + 9 + zz, ROWS - 1)
                 if need >= rows_done:
                     break
                 if zz == 0:
-                    fins[(pi, blk)] = finp.tile([P, 9, ROWS], F32, tag="fin", name="fin%d_%d" % (pi, blk))
+                    fins[(pi, blk)] = finp.tile([P, 9, ROWS + 1], F32, tag="fin", name="fin%d_%d" % (pi, blk))
                 nc.tensor.matmul(
                     out=fins[(pi, blk)][:, zz, :],
                     lhsT=raccs[pi % 2][:, z * P : (z + 1) * P],
@@ -190,8 +195,8 @@ def tile_conv2d_t_kernel(tc, x, weights, bias, grad_out, out):
                 if blk == 0:
                     otiles[pi] = outp.tile([P, ZT * ROWS], F32, tag="o", name="o%d" % pi)
                 nc.scalar.copy(
-                    out=otiles[pi][:, 315 * blk : 315 * blk + 315],
-                    in_=fins[(pi, blk)][:].rearrange("p z w -> p (z w)"),
+                    out=otiles[pi][:, 315 * blk : 315 * blk + 315].rearrange("p (z w) -> p z w", w=ROWS),
+                    in_=fins[(pi, blk)][:, :, 0:ROWS],
                 )
                 pending_st.append((pi, blk))
             state["e2"] = len(pending_e2)
@@ -239,10 +244,12 @@ def tile_conv2d_t_kernel(tc, x, weights, bias, grad_out, out):
                         stop=(npass[om] == 7),
                     )
                     npass[om] += 1
+                    if di % FM_EVERY == FM_EVERY - 1:
+                        final_upto(state["rows"], 1)
+                state["rows"] = state["next_rows"]
                 if npass[om] == 8:
                     evacuate(om)
-                    final_upto(state["rows"])
-                    state["rows"] = 8 * om + 8
+                    state["next_rows"] = 8 * om + 8
                 nextwin[kp] += 1
 
         load_w(0)
@@ -294,5 +301,5 @@ def tile_conv2d_t_kernel(tc, x, weights, bias, grad_out, out):
                 multiply(n - 1)
             if n == 1:
                 w_transposes(1)
-        final_upto(PAIRS * ROWS + 4)
+        final_upto(PAIRS * ROWS + 4, PAIRS * ZT)
         flush_e2()

@@ -21,17 +21,14 @@ ROWS = 35
 RC = 64
 NIN = 147
 NWIN = 18
-ZT = 18
 UNITS = 16
 GROUPS = 8
 AHEAD = 3
-S_SLICES = (2, 1, 2, 2)
-S_SLICES_LAST = {0: 2, 15: 2}
-EARLY = 2
-FM_EVERY = 1
-SA = 0
-GBUFS = 4
+WPAD = 36
+S_ROWS = (2, 2, 2, 2)
+S_ROWS_AT = {0: 2, 15: 2}
 SPLIT_Q = (0, 15)
+EARLY = 2
 
 
 def tile_conv2d_t_kernel(tc, x, weights, bias, grad_out, out):
@@ -40,8 +37,8 @@ def tile_conv2d_t_kernel(tc, x, weights, bias, grad_out, out):
         ctx.enter_context(tc.manual_schedule())
         keep = ctx.enter_context(tc.tile_pool(name="keep", bufs=1))
         rawp = ctx.enter_context(tc.tile_pool(name="rawp", bufs=2 * AHEAD))
-        grpp = ctx.enter_context(tc.tile_pool(name="grpp", bufs=GBUFS))
-        outp = ctx.enter_context(tc.tile_pool(name="outp", bufs=4))
+        grpp = ctx.enter_context(tc.tile_pool(name="grpp", bufs=4))
+        hlp = ctx.enter_context(tc.tile_pool(name="hlp", bufs=4))
         accp = ctx.enter_context(tc.psum_pool(name="accp", bufs=6))
         finp = ctx.enter_context(tc.psum_pool(name="finp", bufs=2))
 
@@ -54,10 +51,9 @@ def tile_conv2d_t_kernel(tc, x, weights, bias, grad_out, out):
         wraws = [wraw_a, wraw_b]
         wg = keep.tile([P, 4096], BF16, align_bytes=64)
         ident = keep.tile([P, P], F32)
-        cmat = keep.tile([P, ROWS + 1], F32)
-        racc_a = keep.tile([P, ZT * P], F32)
-        racc_b = keep.tile([P, ZT * P], F32)
-        raccs = [racc_a, racc_b]
+        cmat = keep.tile([P, WPAD], F32)
+        cbf = keep.tile([P, WPAD], BF16)
+        oall = keep.tile([P, NWIN, 4, ROWS], F32)
         out2 = out.rearrange("b c h w -> (b c) (h w)")
 
         raws = {}
@@ -120,7 +116,7 @@ def tile_conv2d_t_kernel(tc, x, weights, bias, grad_out, out):
                 raws[(grp, be)][:].rearrange("p (j c a f) -> p a c j f", j=4, c=32, a=8, f=4)
                 for be in range(2)
             ]
-            return g6, r5, 4 * half, 4 - S_SLICES_LAST.get(s, S_SLICES[s % 4])
+            return g6, r5, 4 * half, 4 - S_ROWS_AT.get(s, S_ROWS[s % 4])
 
         def regroup_v(s):
             g6, r5, a0, first = views(s)
@@ -149,73 +145,73 @@ def tile_conv2d_t_kernel(tc, x, weights, bias, grad_out, out):
         accs = {}
         npass = {}
         nextwin = [0, 0]
+        his = {}
+        los = {}
         fins = {}
-        otiles = {}
-        state = {"zdone": 0, "rows": 0, "loads": AHEAD, "e2": 0, "st": 0, "next_rows": 0}
-        pending_e2 = []
-        pending_st = []
+        closed = []
+        state = {"loads": AHEAD, "lo": 0, "fm": 0, "fm_ok": 0, "e2": 0, "st": 0}
 
-        def final_upto(rows_done, limit):
-            count = 0
-            while state["zdone"] < PAIRS * ZT and count < limit:
-                count += 1
-                pi, z = divmod(state["zdone"], ZT)
-                blk, zz = divmod(z, 9)
-                need = ROWS * pi + min(18 * blk + 9 + zz, ROWS - 1)
-                if need >= rows_done:
-                    break
-                if zz == 0:
-                    fins[(pi, blk)] = finp.tile([P, 9, ROWS + 1], F32, tag="fin", name="fin%d_%d" % (pi, blk))
-                nc.tensor.matmul(
-                    out=fins[(pi, blk)][:, zz, :],
-                    lhsT=raccs[pi % 2][:, z * P : (z + 1) * P],
-                    rhs=cmat[:],
-                    start=True,
-                    stop=True,
+        def split_view(ap):
+            return ap.rearrange("p (t y c) -> p y t c", y=2, c=RC)
+
+        def hi_copy(om):
+            his[om] = hlp.tile([P, 512], BF16, tag="hi", name="hi%d" % om)
+            nc.scalar.copy(
+                out=split_view(his[om][:]),
+                in_=accs[om][:].rearrange("p (y t c) -> p y t c", y=2, c=RC),
+            )
+            closed.append(om)
+
+        def lo_all():
+            for om in closed[state["lo"] :]:
+                los[om] = hlp.tile([P, 512], BF16, tag="lo", name="lo%d" % om)
+                nc.vector.tensor_tensor(
+                    out=split_view(los[om][:]),
+                    in0=accs[om][:].rearrange("p (y t c) -> p y t c", y=2, c=RC),
+                    in1=split_view(his[om][:]),
+                    op=mybir.AluOpType.subtract,
                 )
-                if zz == 8:
-                    pending_e2.append((pi, blk))
-                state["zdone"] += 1
+            state["lo"] = len(closed)
 
-        def flush_st():
+        def final_tiles(limit):
+            count = 0
+            while state["fm"] < 4 * state["fm_ok"] and count < limit:
+                k, t = divmod(state["fm"], 4)
+                om = closed[k]
+                if om % 3 == 0 and t == 0:
+                    fins[om // 3] = finp.tile([P, 3, 4, WPAD], F32, tag="fin", name="fin%d" % (om // 3))
+                for part in range(2):
+                    nc.tensor.matmul(
+                        out=fins[om // 3][:, om % 3, t, :],
+                        lhsT=(his, los)[part][om][:, t * P : (t + 1) * P],
+                        rhs=cbf[:],
+                        start=(part == 0),
+                        stop=(part == 1),
+                    )
+                state["fm"] += 1
+                count += 1
+
+        def stores():
             if state["loads"] < GROUPS:
                 return
-            for pi, blk in pending_st[state["st"] :]:
+            for om in closed[state["st"] : state["e2"]]:
                 for y2 in range(2):
-                    n = 315 if 18 * blk + 9 * y2 + 9 <= ROWS else 280
-                    col = (18 * blk + 9 * y2) * ROWS
-                    nc.sync.dma_start(
-                        out=out2[64 * pi : 64 * pi + 64, col : col + n],
-                        in_=otiles[pi][64 * y2 : 64 * y2 + 64, 315 * blk : 315 * blk + n],
-                    )
-            state["st"] = len(pending_st)
+                    t = 0
+                    while t < 4 and 8 * om + 4 * y2 + t < PAIRS * ROWS:
+                        pi, h = divmod(8 * om + 4 * y2 + t, ROWS)
+                        n = min(4 - t, ROWS - h)
+                        nc.sync.dma_start(
+                            out=out2[64 * pi : 64 * pi + 64, h * ROWS : (h + n) * ROWS],
+                            in_=oall[64 * y2 : 64 * y2 + 64, om, t : t + n, :].rearrange("p t w -> p (t w)"),
+                        )
+                        t += n
+            state["st"] = state["e2"]
 
-        def flush_e2():
-            for pi, blk in pending_e2[state["e2"] :]:
-                if blk == 0:
-                    otiles[pi] = outp.tile([P, ZT * ROWS], F32, tag="o", name="o%d" % pi)
-                nc.scalar.copy(
-                    out=otiles[pi][:, 315 * blk : 315 * blk + 315].rearrange("p (z w) -> p z w", w=ROWS),
-                    in_=fins[(pi, blk)][:, :, 0:ROWS],
-                )
-                pending_st.append((pi, blk))
-            state["e2"] = len(pending_e2)
-            flush_st()
-
-        def evacuate(om):
-            r = 0
-            while r < 8 and 8 * om + r < PAIRS * ROWS:
-                pi, h = divmod(8 * om + r, ROWS)
-                n = min(8 - r, 9 - h % 9, ROWS - h)
-                blk, hh = divmod(h, 18)
-                y2, zz = divmod(hh, 9)
-                z0 = 9 * blk + zz
-                dst = raccs[pi % 2][:].rearrange("p (z y c) -> p z y c", y=2, c=RC)
-                nc.scalar.copy(
-                    out=dst[:, z0 : z0 + n, y2, :],
-                    in_=accs[om][:, r * RC : (r + n) * RC].rearrange("p (r c) -> p r c", c=RC),
-                )
-                r += n
+        def copy_out():
+            for om in closed[state["e2"] : state["fm"] // 4]:
+                nc.scalar.copy(out=oall[:, om, :, :], in_=fins[om // 3][:, om % 3, :, 0:ROWS])
+            state["e2"] = state["fm"] // 4
+            stores()
 
         def multiply(s):
             grp, half = divmod(s, 2)
@@ -244,12 +240,13 @@ def tile_conv2d_t_kernel(tc, x, weights, bias, grad_out, out):
                         stop=(npass[om] == 7),
                     )
                     npass[om] += 1
-                    if di % FM_EVERY == FM_EVERY - 1:
-                        final_upto(state["rows"], 1)
-                state["rows"] = state["next_rows"]
+                    final_tiles(1)
+                if s == UNITS - 1:
+                    state["fm_ok"] = state["lo"]
                 if npass[om] == 8:
-                    evacuate(om)
-                    state["next_rows"] = 8 * om + 8
+                    hi_copy(om)
+                    if s == UNITS - 1:
+                        lo_all()
                 nextwin[kp] += 1
 
         load_w(0)
@@ -263,8 +260,6 @@ def tile_conv2d_t_kernel(tc, x, weights, bias, grad_out, out):
             g1 = g0 + 3 if pi < PAIRS else NIN
             nc.vector.memset(codes[:, :, g0 * RC : g1 * RC].bitcast(I32), 0)
             nc.vector.memset(scl[:, :, g0 * RC : g1 * RC].bitcast(I32), 0)
-        for racc in raccs:
-            nc.vector.memset(racc[:, (ZT - 1) * P + RC : ZT * P], 0.0)
         nc.vector.memset(cmat[:], 0.0)
         for dj in range(4):
             nc.vector.tensor_tensor(
@@ -273,22 +268,23 @@ def tile_conv2d_t_kernel(tc, x, weights, bias, grad_out, out):
                 in1=ident[:, 32 * dj : 32 * dj + 32],
                 op=mybir.AluOpType.add,
             )
+        nc.vector.tensor_copy(out=cbf[:], in_=cmat[:])
         w_transposes(0)
         w_copies(0)
         w_quantise(0)
         regroup_v(0)
-        for s in range(SA + 1):
-            regroup_s(s)
+        regroup_s(0)
         quantise(0)
         for n in range(UNITS + 1):
-            flush_e2()
+            copy_out()
+            lo_all()
+            state["fm_ok"] = state["lo"]
             if n == 2:
                 w_copies(1)
             if 1 <= n < EARLY:
                 quantise(n)
-            if n + 1 + SA < UNITS:
-                regroup_s(n + 1 + SA)
             if n + 1 < UNITS:
+                regroup_s(n + 1)
                 regroup_v(n + 1)
                 if n % 2 == 0 and state["loads"] < GROUPS:
                     load_group(state["loads"])
@@ -301,5 +297,6 @@ def tile_conv2d_t_kernel(tc, x, weights, bias, grad_out, out):
                 multiply(n - 1)
             if n == 1:
                 w_transposes(1)
-        final_upto(PAIRS * ROWS + 4, PAIRS * ZT)
-        flush_e2()
+        state["fm_ok"] = state["lo"]
+        final_tiles(4 * NWIN)
+        copy_out()

@@ -25,7 +25,7 @@ UNITS = 16
 GROUPS = 8
 AHEAD = 3
 WPAD = 36
-S_ROWS = (2, 2, 2, 2)
+S_ROWS = (1, 2, 2, 2)
 S_ROWS_AT = {0: 2, 15: 2}
 SPLIT_Q = (0, 15)
 EARLY = 2

@@ -46,6 +46,8 @@ def tile_conv2d_t_kernel(tc, x, weights, bias, grad_out, out):
         scl = keep.tile([P, KP, NIN * RC], U8, align_bytes=64)
         wc = keep.tile([P, KP * 512], U32, align_bytes=64)
         ws = keep.tile([P, KP * 512], U8, align_bytes=64)
+        wcn = keep.tile([P, KP * 512], U32, align_bytes=64)
+        wsn = keep.tile([P, KP * 512], U8, align_bytes=64)
         wraw_a = keep.tile([P, 4, 512], BF16)
         wraw_b = keep.tile([P, 4, 512], BF16)
         wraws = [wraw_a, wraw_b]
@@ -59,12 +61,10 @@ def tile_conv2d_t_kernel(tc, x, weights, bias, grad_out, out):
         raws = {}
 
         def load_w(kp):
-            wsrc = weights.rearrange("(j di dj) k -> dj j di k", di=4, dj=4)
-            for dj in range(4):
-                nc.sync.dma_start(
-                    out=wraws[kp][32 * dj : 32 * dj + 32],
-                    in_=wsrc[dj][:, :, kp * 512 : (kp + 1) * 512],
-                )
+            nc.sync.dma_start(
+                out=wraws[kp][:],
+                in_=weights.rearrange("(blk r) k -> r blk k", r=P)[:, :, kp * 512 : (kp + 1) * 512],
+            )
 
         def load_group(grp):
             pi, kp = divmod(grp, KP)
@@ -80,7 +80,7 @@ def tile_conv2d_t_kernel(tc, x, weights, bias, grad_out, out):
         wg32 = wg[:].bitcast(F32).rearrange("p (kp di m e) -> p kp di m e", kp=2, di=4, e=2)
 
         def w_transposes(kp):
-            w32 = wraws[kp][:].rearrange("p di k -> p (di k)").bitcast(F32)
+            w32 = wraws[kp][:].rearrange("p blk k -> p (blk k)").bitcast(F32)
             for dp in range(2):
                 wt = accp.tile([P, 4, P], F32, tag="acc", name="wt%d_%d" % (kp, dp))
                 for d in range(2):
@@ -99,10 +99,19 @@ def tile_conv2d_t_kernel(tc, x, weights, bias, grad_out, out):
                     nc.scalar.copy(out=dst, in_=src)
 
         def w_quantise(kp):
+            cols = slice(kp * 512, (kp + 1) * 512)
             nc.vector.quantize_mx(
-                out=wc[:, kp * 512 : (kp + 1) * 512].bitcast(E4X4),
-                scales=ws[:, kp * 512 : (kp + 1) * 512],
+                out=wcn[:, cols].bitcast(E4X4),
+                scales=wsn[:, cols],
                 in_=wg[:, kp * 2048 : (kp + 1) * 2048],
+            )
+            nc.vector.tensor_copy(
+                out=wc[:, cols].bitcast(I32).rearrange("p (di j dj) -> p di j dj", di=4, dj=4),
+                in_=wcn[:, cols].bitcast(I32).rearrange("p (j di dj) -> p di j dj", di=4, dj=4),
+            )
+            nc.vector.tensor_copy(
+                out=ws[:, cols].bitcast(I32).rearrange("p (di j) -> p di j", di=4),
+                in_=wsn[:, cols].bitcast(I32).rearrange("p (j di) -> p di j", di=4),
             )
 
         ggs = {}
@@ -260,12 +269,13 @@ def tile_conv2d_t_kernel(tc, x, weights, bias, grad_out, out):
             g1 = g0 + 3 if pi < PAIRS else NIN
             nc.vector.memset(codes[:, :, g0 * RC : g1 * RC].bitcast(I32), 0)
             nc.vector.memset(scl[:, :, g0 * RC : g1 * RC].bitcast(I32), 0)
+        nc.vector.memset(wsn[:].bitcast(I32), 0)
         nc.vector.memset(cmat[:], 0.0)
         for dj in range(4):
             nc.vector.tensor_tensor(
                 out=cmat[:, dj : dj + 32],
                 in0=cmat[:, dj : dj + 32],
-                in1=ident[:, 32 * dj : 32 * dj + 32],
+                in1=ident[:, dj:P:4],
                 op=mybir.AluOpType.add,
             )
         nc.vector.tensor_copy(out=cbf[:], in_=cmat[:])

@@ -34,7 +34,6 @@ EARLY = 2
 def tile_conv2d_t_kernel(tc, x, weights, bias, grad_out, out):
     nc = tc.nc
     with ExitStack() as ctx:
-        ctx.enter_context(tc.manual_schedule())
         keep = ctx.enter_context(tc.tile_pool(name="keep", bufs=1))
         rawp = ctx.enter_context(tc.tile_pool(name="rawp", bufs=2 * AHEAD))
         grpp = ctx.enter_context(tc.tile_pool(name="grpp", bufs=4))

@@ -11,301 +11,257 @@ F32 = mybir.dt.float32
 I32 = mybir.dt.int32
 U32 = mybir.dt.uint32
 U8 = mybir.dt.uint8
-E4X4 = mybir.dt.float8_e4m3fn_x4
-E5X4 = mybir.dt.float8_e5m2_x4
+E4M3X4 = mybir.dt.float8_e4m3fn_x4
+E5M2X4 = mybir.dt.float8_e5m2_x4
 
 P = 128
+K_PASS = 512
+HALVES = 2
+KS = 4
+TOKENS = 1024
+IMG = 35
 PAIRS = 4
-KP = 2
-ROWS = 35
-RC = 64
-NIN = 147
-NWIN = 18
-UNITS = 16
-GROUPS = 8
-AHEAD = 3
-WPAD = 36
-S_ROWS = (1, 2, 2, 2)
-S_ROWS_AT = {0: 2, 15: 2}
-SPLIT_Q = (0, 15)
-EARLY = 2
+ROW = 64
+PAD = KS - 1
+WIN = 8
+OUT_ROWS = PAIRS * IMG
+WINDOWS = (OUT_ROWS + WIN - 1) // WIN
+IN_ROWS = WINDOWS * WIN + PAD
+UNIT = 16
+UNITS = PAIRS * HALVES * 2
+CHUNKS_AHEAD = 6
+W_COLS = IMG + 1
+BANK_WINDOWS = 3
+SCALAR_GROUPS = (1, 2, 2, 2)
+IN_TWO_CALLS = (0, UNITS - 1)
 
 
 def tile_conv2d_t_kernel(tc, x, weights, bias, grad_out, out):
     nc = tc.nc
     with ExitStack() as ctx:
         keep = ctx.enter_context(tc.tile_pool(name="keep", bufs=1))
-        rawp = ctx.enter_context(tc.tile_pool(name="rawp", bufs=2 * AHEAD))
-        grpp = ctx.enter_context(tc.tile_pool(name="grpp", bufs=4))
-        hlp = ctx.enter_context(tc.tile_pool(name="hlp", bufs=4))
-        accp = ctx.enter_context(tc.psum_pool(name="accp", bufs=6))
-        finp = ctx.enter_context(tc.psum_pool(name="finp", bufs=2))
+        chunks = ctx.enter_context(tc.tile_pool(name="chunks", bufs=CHUNKS_AHEAD))
+        work = ctx.enter_context(tc.tile_pool(name="work", bufs=4))
+        banks = ctx.enter_context(tc.psum_pool(name="banks", bufs=6))
+        result_banks = ctx.enter_context(tc.psum_pool(name="result_banks", bufs=2))
 
-        codes = keep.tile([P, KP, NIN * RC], U32, align_bytes=64)
-        scl = keep.tile([P, KP, NIN * RC], U8, align_bytes=64)
-        wc = keep.tile([P, KP * 512], U32, align_bytes=64)
-        ws = keep.tile([P, KP * 512], U8, align_bytes=64)
-        wcn = keep.tile([P, KP * 512], U32, align_bytes=64)
-        wsn = keep.tile([P, KP * 512], U8, align_bytes=64)
-        wraw_a = keep.tile([P, 4, 512], BF16)
-        wraw_b = keep.tile([P, 4, 512], BF16)
-        wraws = [wraw_a, wraw_b]
-        wg = keep.tile([P, 4096], BF16, align_bytes=64)
+        g_words = keep.tile([P, HALVES, IN_ROWS * ROW], U32, align_bytes=64)
+        g_scales = keep.tile([P, HALVES, IN_ROWS * ROW], U8, align_bytes=64)
+        w_words = keep.tile([P, HALVES * K_PASS], U32, align_bytes=64)
+        w_scales = keep.tile([P, HALVES * K_PASS], U8, align_bytes=64)
+        w_words_asis = keep.tile([P, HALVES * K_PASS], U32, align_bytes=64)
+        w_scales_asis = keep.tile([P, HALVES * K_PASS], U8, align_bytes=64)
+        w_rows_0 = keep.tile([P, 4, K_PASS], BF16)
+        w_rows_1 = keep.tile([P, 4, K_PASS], BF16)
+        w_rows = [w_rows_0, w_rows_1]
+        w_grouped = keep.tile([P, HALVES * K_PASS * 4], BF16, align_bytes=64)
         ident = keep.tile([P, P], F32)
-        cmat = keep.tile([P, WPAD], F32)
-        cbf = keep.tile([P, WPAD], BF16)
-        oall = keep.tile([P, NWIN, 4, ROWS], F32)
-        out2 = out.rearrange("b c h w -> (b c) (h w)")
+        fold_f32 = keep.tile([P, W_COLS], F32)
+        fold = keep.tile([P, W_COLS], BF16)
+        results = keep.tile([P, WINDOWS, 4, IMG], F32)
+        out_rows = out.rearrange("b c h w -> (b c) (h w)")
 
-        raws = {}
 
-        def load_w(kp):
+        def load_weights(half):
             nc.sync.dma_start(
-                out=wraws[kp][:],
-                in_=weights.rearrange("(blk r) k -> r blk k", r=P)[:, :, kp * 512 : (kp + 1) * 512],
+                out=w_rows[half][:],
+                in_=weights.rearrange("(blk r) k -> r blk k", r=P)[:, :, half * K_PASS : (half + 1) * K_PASS],
             )
 
-        def load_group(grp):
-            pi, kp = divmod(grp, KP)
-            for be in range(2):
-                raw = rawp.tile([P, 4096], BF16, tag="raw", name="raw%d_%d" % (grp, be))
-                nc.sync.dma_start(
-                    out=raw[:],
-                    in_=grad_out[2 * pi + be, kp * 512 : (kp + 1) * 512].rearrange("(p j) u v -> p (j u v)", j=4),
-                )
-                raws[(grp, be)] = raw
-
-        wts = {}
-        wg32 = wg[:].bitcast(F32).rearrange("p (kp di m e) -> p kp di m e", kp=2, di=4, e=2)
-
-        def w_transposes(kp):
-            w32 = wraws[kp][:].rearrange("p blk k -> p (blk k)").bitcast(F32)
-            for dp in range(2):
-                wt = accp.tile([P, 4, P], F32, tag="acc", name="wt%d_%d" % (kp, dp))
-                for d in range(2):
+        def prepare_weights(half):
+            words = w_rows[half][:].rearrange("p blk k -> p (blk k)").bitcast(F32)
+            w_pairs = w_grouped[:].bitcast(F32).rearrange("p (h blk r e) -> p h blk r e", h=HALVES, blk=4, e=2)
+            turned = []
+            for two in range(2):
+                turned.append(banks.tile([P, 4, P], F32, tag="bank", name="turned%d_%d" % (half, two)))
+                for blk in range(2):
                     for e in range(2):
-                        s = (2 * dp + d) * 256 + e
-                        nc.tensor.transpose(wt[:, 2 * d + e, :], w32[:, s : s + 255 : 2], ident[:])
-                wts[(kp, dp)] = wt
-
-        def w_copies(kp):
-            for dp in range(2):
-                src = wts[(kp, dp)][:].rearrange("p (d e) m -> p d m e", e=2)
-                dst = wg32[:, kp, 2 * dp : 2 * dp + 2, :, :]
-                if dp == 0:
-                    nc.vector.tensor_copy(out=dst, in_=src)
-                else:
-                    nc.scalar.copy(out=dst, in_=src)
-
-        def w_quantise(kp):
-            cols = slice(kp * 512, (kp + 1) * 512)
-            nc.vector.quantize_mx(
-                out=wcn[:, cols].bitcast(E4X4),
-                scales=wsn[:, cols],
-                in_=wg[:, kp * 2048 : (kp + 1) * 2048],
-            )
-            nc.vector.tensor_copy(
-                out=wc[:, cols].bitcast(I32).rearrange("p (di j dj) -> p di j dj", di=4, dj=4),
-                in_=wcn[:, cols].bitcast(I32).rearrange("p (j di dj) -> p di j dj", di=4, dj=4),
-            )
-            nc.vector.tensor_copy(
-                out=ws[:, cols].bitcast(I32).rearrange("p (di j) -> p di j", di=4),
-                in_=wsn[:, cols].bitcast(I32).rearrange("p (j di) -> p di j", di=4),
-            )
-
-        ggs = {}
-
-        def views(s):
-            grp, half = divmod(s, 2)
-            if s not in ggs:
-                ggs[s] = grpp.tile([P, 4096], BF16, tag="grp", align_bytes=64, name="gg%d" % s)
-            g6 = ggs[s][:].rearrange("p (a f b c j) -> p b a c j f", a=4, f=4, b=2, c=32, j=4)
-            r5 = [
-                raws[(grp, be)][:].rearrange("p (j c a f) -> p a c j f", j=4, c=32, a=8, f=4)
-                for be in range(2)
-            ]
-            return g6, r5, 4 * half, 4 - S_ROWS_AT.get(s, S_ROWS[s % 4])
-
-        def regroup_v(s):
-            g6, r5, a0, first = views(s)
-            for be in range(2):
-                nc.vector.tensor_copy(out=g6[:, be, 0:first], in_=r5[be][:, a0 : a0 + first])
-
-        def regroup_s(s):
-            g6, r5, a0, first = views(s)
-            for a in range(first, 4):
-                for be in range(2):
-                    nc.scalar.copy(out=g6[:, be, a], in_=r5[be][:, a0 + a])
-
-        def quantise(s):
-            grp, half = divmod(s, 2)
-            pi, kp = divmod(grp, KP)
-            c0 = (ROWS * pi + 3 + 16 * half) * RC
-            parts = 2 if s in SPLIT_Q else 1
-            wid = 1024 // parts
-            for q in range(parts):
-                nc.vector.quantize_mx(
-                    out=codes[:, kp, c0 + q * wid : c0 + (q + 1) * wid].bitcast(E5X4),
-                    scales=scl[:, kp, c0 + q * wid : c0 + (q + 1) * wid],
-                    in_=ggs[s][:, 4 * q * wid : 4 * (q + 1) * wid],
-                )
-
-        accs = {}
-        npass = {}
-        nextwin = [0, 0]
-        his = {}
-        los = {}
-        fins = {}
-        closed = []
-        state = {"loads": AHEAD, "lo": 0, "fm": 0, "fm_ok": 0, "e2": 0, "st": 0}
-
-        def split_view(ap):
-            return ap.rearrange("p (t y c) -> p y t c", y=2, c=RC)
-
-        def hi_copy(om):
-            his[om] = hlp.tile([P, 512], BF16, tag="hi", name="hi%d" % om)
-            nc.scalar.copy(
-                out=split_view(his[om][:]),
-                in_=accs[om][:].rearrange("p (y t c) -> p y t c", y=2, c=RC),
-            )
-            closed.append(om)
-
-        def lo_all():
-            for om in closed[state["lo"] :]:
-                los[om] = hlp.tile([P, 512], BF16, tag="lo", name="lo%d" % om)
-                nc.vector.tensor_tensor(
-                    out=split_view(los[om][:]),
-                    in0=accs[om][:].rearrange("p (y t c) -> p y t c", y=2, c=RC),
-                    in1=split_view(his[om][:]),
-                    op=mybir.AluOpType.subtract,
-                )
-            state["lo"] = len(closed)
-
-        def final_tiles(limit):
-            count = 0
-            while state["fm"] < 4 * state["fm_ok"] and count < limit:
-                k, t = divmod(state["fm"], 4)
-                om = closed[k]
-                if om % 3 == 0 and t == 0:
-                    fins[om // 3] = finp.tile([P, 3, 4, WPAD], F32, tag="fin", name="fin%d" % (om // 3))
-                for part in range(2):
-                    nc.tensor.matmul(
-                        out=fins[om // 3][:, om % 3, t, :],
-                        lhsT=(his, los)[part][om][:, t * P : (t + 1) * P],
-                        rhs=cbf[:],
-                        start=(part == 0),
-                        stop=(part == 1),
-                    )
-                state["fm"] += 1
-                count += 1
-
-        def stores():
-            if state["loads"] < GROUPS:
-                return
-            for om in closed[state["st"] : state["e2"]]:
-                for y2 in range(2):
-                    t = 0
-                    while t < 4 and 8 * om + 4 * y2 + t < PAIRS * ROWS:
-                        pi, h = divmod(8 * om + 4 * y2 + t, ROWS)
-                        n = min(4 - t, ROWS - h)
-                        nc.sync.dma_start(
-                            out=out2[64 * pi : 64 * pi + 64, h * ROWS : (h + n) * ROWS],
-                            in_=oall[64 * y2 : 64 * y2 + 64, om, t : t + n, :].rearrange("p t w -> p (t w)"),
+                        word = (2 * two + blk) * (K_PASS // 2) + e
+                        nc.tensor.transpose(
+                            turned[two][:, 2 * blk + e, :], words[:, word : word + K_PASS // 2 - 1 : 2], ident[:]
                         )
-                        t += n
-            state["st"] = state["e2"]
+            nc.vector.tensor_copy(
+                out=w_pairs[:, half, 0:2, :, :], in_=turned[0][:].rearrange("p (blk e) r -> p blk r e", e=2)
+            )
+            nc.scalar.copy(
+                out=w_pairs[:, half, 2:4, :, :], in_=turned[1][:].rearrange("p (blk e) r -> p blk r e", e=2)
+            )
+            cols = slice(half * K_PASS, (half + 1) * K_PASS)
+            nc.vector.quantize_mx(
+                out=w_words_asis[:, cols].bitcast(E4M3X4),
+                scales=w_scales_asis[:, cols],
+                in_=w_grouped[:, half * K_PASS * 4 : (half + 1) * K_PASS * 4],
+            )
+            nc.vector.tensor_copy(
+                out=w_words[:, cols].bitcast(I32).rearrange("p (di j dj) -> p di j dj", di=KS, dj=KS),
+                in_=w_words_asis[:, cols].bitcast(I32).rearrange("p (j di dj) -> p di j dj", di=KS, dj=KS),
+            )
+            nc.vector.tensor_copy(
+                out=w_scales[:, cols].bitcast(I32).rearrange("p (di j) -> p di j", di=KS),
+                in_=w_scales_asis[:, cols].bitcast(I32).rearrange("p (j di) -> p di j", di=KS),
+            )
 
-        def copy_out():
-            for om in closed[state["e2"] : state["fm"] // 4]:
-                nc.scalar.copy(out=oall[:, om, :, :], in_=fins[om // 3][:, om % 3, :, 0:ROWS])
-            state["e2"] = state["fm"] // 4
-            stores()
 
-        def multiply(s):
-            grp, half = divmod(s, 2)
-            pi, kp = divmod(grp, KP)
-            if half == 0:
-                avail = ROWS * pi + 3 + 16
-            elif pi < PAIRS - 1:
-                avail = ROWS * (pi + 1) + 3
-            else:
-                avail = NIN
-            while nextwin[kp] < NWIN and 8 * nextwin[kp] + 10 < avail:
-                om = nextwin[kp]
-                if om not in accs:
-                    accs[om] = accp.tile([P, 512], F32, tag="acc", name="acc%d" % om)
-                    npass[om] = 0
-                for di in range(4):
-                    c0 = (8 * om + 3 - di) * RC
-                    o = kp * 512 + di * P
-                    nc.tensor.matmul_mx(
-                        out=accs[om][:],
-                        lhsT=wc[:, o : o + P].bitcast(E4X4),
-                        lhsT_scale=ws[:, o : o + P],
-                        rhs=codes[:, kp, c0 : c0 + 512].bitcast(E5X4),
-                        rhs_scale=scl[:, kp, c0 : c0 + 512],
-                        start=(npass[om] == 0),
-                        stop=(npass[om] == 7),
+        loaded = {}
+
+        def load_pair(pair, half):
+            for b in range(2):
+                chunk = chunks.tile([P, 4 * TOKENS], BF16, tag="chunk", name="chunk%d_%d_%d" % (pair, half, b))
+                nc.sync.dma_start(
+                    out=chunk[:],
+                    in_=grad_out[2 * pair + b, half * K_PASS : (half + 1) * K_PASS].rearrange(
+                        "(p t) c i -> p (t c i)", t=4
+                    ),
+                )
+                loaded[(pair, half, b)] = chunk
+
+        regrouped = {}
+
+        def regroup_unit(unit):
+            pair, rest = divmod(unit, 2 * HALVES)
+            half, part = divmod(rest, 2)
+            grouped = work.tile([P, UNIT * ROW * 4], BF16, tag="grouped", align_bytes=64, name="grouped%d" % unit)
+            target = grouped[:].rearrange("p (g f b c t) -> p b g c t f", g=4, f=4, b=2, t=4)
+            regrouped[unit] = grouped
+            by_vector = 2 if unit in IN_TWO_CALLS else 4 - SCALAR_GROUPS[rest]
+            for b in range(2):
+                source = loaded[(pair, half, b)][:].rearrange("p (t c g f) -> p g c t f", t=4, g=8, f=4)
+                nc.vector.tensor_copy(
+                    out=target[:, b, 0:by_vector], in_=source[:, 4 * part : 4 * part + by_vector]
+                )
+            for g in range(by_vector, 4):
+                for b in range(2):
+                    source = loaded[(pair, half, b)][:].rearrange("p (t c g f) -> p g c t f", t=4, g=8, f=4)
+                    nc.scalar.copy(out=target[:, b, g], in_=source[:, 4 * part + g])
+
+        def quantise_unit(unit):
+            pair, rest = divmod(unit, 2 * HALVES)
+            half, part = divmod(rest, 2)
+            calls = 2 if unit in IN_TWO_CALLS else 1
+            width = UNIT * ROW // calls
+            for call in range(calls):
+                col = (IMG * pair + PAD + UNIT * part) * ROW + call * width
+                nc.vector.quantize_mx(
+                    out=g_words[:, half, col : col + width].bitcast(E5M2X4),
+                    scales=g_scales[:, half, col : col + width],
+                    in_=regrouped[unit][:, 4 * call * width : 4 * (call + 1) * width],
+                )
+
+
+        sums = {}
+        passes_done = {}
+        next_window = [0, 0]
+        result_bank = {}
+        finished = []
+        saved = [0]
+
+        def save_results():
+            for window in finished[saved[0] :]:
+                for upper in range(2):
+                    r = 0
+                    while r < 4 and WIN * window + 4 * upper + r < OUT_ROWS:
+                        pair, h = divmod(WIN * window + 4 * upper + r, IMG)
+                        n = min(4 - r, IMG - h)
+                        nc.sync.dma_start(
+                            out=out_rows[ROW * pair : ROW * (pair + 1), h * IMG : (h + n) * IMG],
+                            in_=results[ROW * upper : ROW * (upper + 1), window, r : r + n, :].rearrange(
+                                "p r w -> p (r w)"
+                            ),
+                        )
+                        r += n
+            saved[0] = len(finished)
+
+        def finish_window(window, all_loads_issued):
+            bank = sums[window][:].rearrange("p (upper r col) -> p upper r col", upper=2, col=ROW)
+            hi = work.tile([P, WIN * ROW], BF16, tag="hi", name="hi%d" % window)
+            lo = work.tile([P, WIN * ROW], BF16, tag="lo", name="lo%d" % window)
+            hi_rows = hi[:].rearrange("p (r upper col) -> p upper r col", upper=2, col=ROW)
+            lo_rows = lo[:].rearrange("p (r upper col) -> p upper r col", upper=2, col=ROW)
+            nc.scalar.copy(out=hi_rows, in_=bank)
+            nc.vector.tensor_tensor(out=lo_rows, in0=bank, in1=hi_rows, op=mybir.AluOpType.subtract)
+            place = window % BANK_WINDOWS
+            if place == 0:
+                result_bank[0] = result_banks.tile(
+                    [P, BANK_WINDOWS, 4, W_COLS], F32, tag="result", name="result%d" % window
+                )
+            for r in range(4):
+                for term in (hi, lo):
+                    nc.tensor.matmul(
+                        out=result_bank[0][:, place, r, :],
+                        lhsT=term[:, r * P : (r + 1) * P],
+                        rhs=fold[:],
+                        start=(term is hi),
+                        stop=(term is lo),
                     )
-                    npass[om] += 1
-                    final_tiles(1)
-                if s == UNITS - 1:
-                    state["fm_ok"] = state["lo"]
-                if npass[om] == 8:
-                    hi_copy(om)
-                    if s == UNITS - 1:
-                        lo_all()
-                nextwin[kp] += 1
+            nc.scalar.copy(out=results[:, window, :, :], in_=result_bank[0][:, place, :, 0:IMG])
+            finished.append(window)
+            if all_loads_issued:
+                save_results()
 
-        load_w(0)
-        load_group(0)
-        load_w(1)
-        load_group(1)
-        load_group(2)
+        def multiply(unit, all_loads_issued):
+            pair, rest = divmod(unit, 2 * HALVES)
+            half, part = divmod(rest, 2)
+            if part == 0:
+                rows_ready = IMG * pair + PAD + UNIT
+            elif pair < PAIRS - 1:
+                rows_ready = IMG * (pair + 1) + PAD
+            else:
+                rows_ready = IN_ROWS
+            while next_window[half] < WINDOWS and WIN * (next_window[half] + 1) + PAD <= rows_ready:
+                window = next_window[half]
+                next_window[half] += 1
+                if window not in sums:
+                    sums[window] = banks.tile([P, WIN * ROW], F32, tag="bank", name="sums%d" % window)
+                    passes_done[window] = 0
+                for di in range(KS):
+                    col = (WIN * window + PAD - di) * ROW
+                    w_col = half * K_PASS + di * P
+                    nc.tensor.matmul_mx(
+                        out=sums[window][:],
+                        lhsT=w_words[:, w_col : w_col + P].bitcast(E4M3X4),
+                        lhsT_scale=w_scales[:, w_col : w_col + P],
+                        rhs=g_words[:, half, col : col + WIN * ROW].bitcast(E5M2X4),
+                        rhs_scale=g_scales[:, half, col : col + WIN * ROW],
+                        start=(passes_done[window] == 0),
+                        stop=(passes_done[window] == HALVES * KS - 1),
+                    )
+                    passes_done[window] += 1
+                if passes_done[window] == HALVES * KS:
+                    finish_window(window, all_loads_issued)
+
+
+        load_order = [(pair, half) for pair in range(PAIRS) for half in range(HALVES)]
+        load_weights(0)
+        load_pair(*load_order[0])
+        load_weights(1)
+        load_pair(*load_order[1])
+        load_pair(*load_order[2])
+        issued = CHUNKS_AHEAD // 2
+
         make_identity(nc, ident[:])
-        for pi in range(PAIRS + 1):
-            g0 = ROWS * pi
-            g1 = g0 + 3 if pi < PAIRS else NIN
-            nc.vector.memset(codes[:, :, g0 * RC : g1 * RC].bitcast(I32), 0)
-            nc.vector.memset(scl[:, :, g0 * RC : g1 * RC].bitcast(I32), 0)
-        nc.vector.memset(wsn[:].bitcast(I32), 0)
-        nc.vector.memset(cmat[:], 0.0)
-        for dj in range(4):
+        for pair in range(PAIRS + 1):
+            col = IMG * pair * ROW
+            end = (IMG * pair + PAD) * ROW if pair < PAIRS else IN_ROWS * ROW
+            nc.vector.memset(g_words[:, :, col:end].bitcast(I32), 0)
+            nc.vector.memset(g_scales[:, :, col:end].bitcast(I32), 0)
+        nc.vector.memset(w_scales_asis[:].bitcast(I32), 0)
+        nc.vector.memset(fold_f32[:], 0.0)
+        for dj in range(KS):
             nc.vector.tensor_tensor(
-                out=cmat[:, dj : dj + 32],
-                in0=cmat[:, dj : dj + 32],
-                in1=ident[:, dj:P:4],
+                out=fold_f32[:, dj : dj + 32],
+                in0=fold_f32[:, dj : dj + 32],
+                in1=ident[:, dj:P:KS],
                 op=mybir.AluOpType.add,
             )
-        nc.vector.tensor_copy(out=cbf[:], in_=cmat[:])
-        w_transposes(0)
-        w_copies(0)
-        w_quantise(0)
-        regroup_v(0)
-        regroup_s(0)
-        quantise(0)
-        for n in range(UNITS + 1):
-            copy_out()
-            lo_all()
-            state["fm_ok"] = state["lo"]
-            if n == 2:
-                w_copies(1)
-            if 1 <= n < EARLY:
-                quantise(n)
-            if n + 1 < UNITS:
-                regroup_s(n + 1)
-                regroup_v(n + 1)
-                if n % 2 == 0 and state["loads"] < GROUPS:
-                    load_group(state["loads"])
-                    state["loads"] += 1
-            if n == 2:
-                w_quantise(1)
-            if EARLY <= n < UNITS:
-                quantise(n)
-            if n >= 1:
-                multiply(n - 1)
-            if n == 1:
-                w_transposes(1)
-        state["fm_ok"] = state["lo"]
-        final_tiles(4 * NWIN)
-        copy_out()
+        nc.vector.tensor_copy(out=fold[:], in_=fold_f32[:])
+        prepare_weights(0)
+
+        for unit in range(UNITS):
+            regroup_unit(unit)
+            if unit % 2 == 1 and issued < len(load_order):
+                load_pair(*load_order[issued])
+                issued += 1
+            quantise_unit(unit)
+            if unit == 1:
+                prepare_weights(1)
+            multiply(unit, issued == len(load_order))

@@ -49,13 +49,12 @@ def tile_conv2d_t_kernel(tc, x, weights, bias, grad_out, out):
         g_scales = keep.tile([P, HALVES, IN_ROWS * ROW], U8, align_bytes=64)
         w_words = keep.tile([P, HALVES * K_PASS], U32, align_bytes=64)
         w_scales = keep.tile([P, HALVES * K_PASS], U8, align_bytes=64)
-        w_words_asis = keep.tile([P, HALVES * K_PASS], U32, align_bytes=64)
-        w_scales_asis = keep.tile([P, HALVES * K_PASS], U8, align_bytes=64)
         w_rows_0 = keep.tile([P, 4, K_PASS], BF16)
         w_rows_1 = keep.tile([P, 4, K_PASS], BF16)
         w_rows = [w_rows_0, w_rows_1]
         w_grouped = keep.tile([P, HALVES * K_PASS * 4], BF16, align_bytes=64)
         ident = keep.tile([P, P], F32)
+        sorter = keep.tile([P, P], F32)
         fold_f32 = keep.tile([P, W_COLS], F32)
         fold = keep.tile([P, W_COLS], BF16)
         results = keep.tile([P, WINDOWS, 4, IMG], F32)
@@ -70,35 +69,27 @@ def tile_conv2d_t_kernel(tc, x, weights, bias, grad_out, out):
 
         def prepare_weights(half):
             words = w_rows[half][:].rearrange("p blk k -> p (blk k)").bitcast(F32)
-            w_pairs = w_grouped[:].bitcast(F32).rearrange("p (h blk r e) -> p h blk r e", h=HALVES, blk=4, e=2)
-            turned = []
+            w_pairs = w_grouped[:].bitcast(F32).rearrange(
+                "p (h di blk s e) -> p h blk di s e", h=HALVES, di=KS, blk=4, e=2
+            )
             for two in range(2):
-                turned.append(banks.tile([P, 4, P], F32, tag="bank", name="turned%d_%d" % (half, two)))
+                turned = banks.tile([P, 4, P], F32, tag="bank", name="turned%d_%d" % (half, two))
                 for blk in range(2):
                     for e in range(2):
                         word = (2 * two + blk) * (K_PASS // 2) + e
                         nc.tensor.transpose(
-                            turned[two][:, 2 * blk + e, :], words[:, word : word + K_PASS // 2 - 1 : 2], ident[:]
+                            turned[:, 2 * blk + e, :], words[:, word : word + K_PASS // 2 - 1 : 2], sorter[:]
                         )
-            nc.vector.tensor_copy(
-                out=w_pairs[:, half, 0:2, :, :], in_=turned[0][:].rearrange("p (blk e) r -> p blk r e", e=2)
-            )
-            nc.scalar.copy(
-                out=w_pairs[:, half, 2:4, :, :], in_=turned[1][:].rearrange("p (blk e) r -> p blk r e", e=2)
-            )
+                for blk in range(2):
+                    nc.scalar.copy(
+                        out=w_pairs[:, half, 2 * two + blk],
+                        in_=turned[:, 2 * blk : 2 * blk + 2, :].rearrange("p e (di s) -> p di s e", di=KS),
+                    )
             cols = slice(half * K_PASS, (half + 1) * K_PASS)
             nc.vector.quantize_mx(
-                out=w_words_asis[:, cols].bitcast(E4M3X4),
-                scales=w_scales_asis[:, cols],
+                out=w_words[:, cols].bitcast(E4M3X4),
+                scales=w_scales[:, cols],
                 in_=w_grouped[:, half * K_PASS * 4 : (half + 1) * K_PASS * 4],
-            )
-            nc.vector.tensor_copy(
-                out=w_words[:, cols].bitcast(I32).rearrange("p (di j dj) -> p di j dj", di=KS, dj=KS),
-                in_=w_words_asis[:, cols].bitcast(I32).rearrange("p (j di dj) -> p di j dj", di=KS, dj=KS),
-            )
-            nc.vector.tensor_copy(
-                out=w_scales[:, cols].bitcast(I32).rearrange("p (di j) -> p di j", di=KS),
-                in_=w_scales_asis[:, cols].bitcast(I32).rearrange("p (j di) -> p di j", di=KS),
             )
 
 
@@ -244,7 +235,10 @@ def tile_conv2d_t_kernel(tc, x, weights, bias, grad_out, out):
             end = (IMG * pair + PAD) * ROW if pair < PAIRS else IN_ROWS * ROW
             nc.vector.memset(g_words[:, :, col:end].bitcast(I32), 0)
             nc.vector.memset(g_scales[:, :, col:end].bitcast(I32), 0)
-        nc.vector.memset(w_scales_asis[:].bitcast(I32), 0)
+        nc.vector.tensor_copy(
+            out=sorter[:].rearrange("p (di j8 dj) -> p di j8 dj", di=KS, dj=KS),
+            in_=ident[:].rearrange("p (j8 di dj) -> p di j8 dj", di=KS, dj=KS),
+        )
         nc.vector.memset(fold_f32[:], 0.0)
         for dj in range(KS):
             nc.vector.tensor_tensor(

@@ -108,22 +108,26 @@ def tile_conv2d_t_kernel(tc, x, weights, bias, grad_out, out):
 
         regrouped = {}
 
-        def regroup_unit(unit):
+        def regroup_unit(unit, engine, batches):
             pair, rest = divmod(unit, 2 * HALVES)
             half, part = divmod(rest, 2)
-            grouped = work.tile([P, UNIT * ROW * 4], BF16, tag="grouped", align_bytes=64, name="grouped%d" % unit)
-            target = grouped[:].rearrange("p (g f b c t) -> p b g c t f", g=4, f=4, b=2, t=4)
-            regrouped[unit] = grouped
-            by_vector = 2 if unit in IN_TWO_CALLS else 4 - SCALAR_GROUPS[rest]
-            for b in range(2):
-                source = loaded[(pair, half, b)][:].rearrange("p (t c g f) -> p g c t f", t=4, g=8, f=4)
-                nc.vector.tensor_copy(
-                    out=target[:, b, 0:by_vector], in_=source[:, 4 * part : 4 * part + by_vector]
+            if unit not in regrouped:
+                regrouped[unit] = work.tile(
+                    [P, UNIT * ROW * 4], BF16, tag="grouped", align_bytes=64, name="grouped%d" % unit
                 )
-            for g in range(by_vector, 4):
-                for b in range(2):
+            target = regrouped[unit][:].rearrange("p (g f b c t) -> p b g c t f", g=4, f=4, b=2, t=4)
+            by_vector = 2 if unit in IN_TWO_CALLS else 4 - SCALAR_GROUPS[rest]
+            if engine == "vector":
+                for b in batches:
                     source = loaded[(pair, half, b)][:].rearrange("p (t c g f) -> p g c t f", t=4, g=8, f=4)
-                    nc.scalar.copy(out=target[:, b, g], in_=source[:, 4 * part + g])
+                    nc.vector.tensor_copy(
+                        out=target[:, b, 0:by_vector], in_=source[:, 4 * part : 4 * part + by_vector]
+                    )
+            else:
+                for g in range(by_vector, 4):
+                    for b in batches:
+                        source = loaded[(pair, half, b)][:].rearrange("p (t c g f) -> p g c t f", t=4, g=8, f=4)
+                        nc.scalar.copy(out=target[:, b, g], in_=source[:, 4 * part + g])
 
         def quantise_unit(unit):
             pair, rest = divmod(unit, 2 * HALVES)
@@ -227,7 +231,7 @@ def tile_conv2d_t_kernel(tc, x, weights, bias, grad_out, out):
         load_weights(1)
         load_pair(*load_order[1])
         load_pair(*load_order[2])
-        issued = CHUNKS_AHEAD // 2
+        issued = [CHUNKS_AHEAD // 2]
 
         make_identity(nc, ident[:])
         for pair in range(PAIRS + 1):
@@ -250,12 +254,19 @@ def tile_conv2d_t_kernel(tc, x, weights, bias, grad_out, out):
         nc.vector.tensor_copy(out=fold[:], in_=fold_f32[:])
         prepare_weights(0)
 
-        for unit in range(UNITS):
-            regroup_unit(unit)
-            if unit % 2 == 1 and issued < len(load_order):
-                load_pair(*load_order[issued])
-                issued += 1
+        def quantise_and_multiply(unit):
             quantise_unit(unit)
             if unit == 1:
                 prepare_weights(1)
-            multiply(unit, issued == len(load_order))
+            multiply(unit, issued[0] == len(load_order))
+
+        for unit in range(UNITS):
+            regroup_unit(unit, "vector", (0,))
+            if unit > 0:
+                quantise_and_multiply(unit - 1)
+            regroup_unit(unit, "vector", (1,))
+            regroup_unit(unit, "scalar", (0, 1))
+            if unit % 2 == 1 and issued[0] < len(load_order):
+                load_pair(*load_order[issued[0]])
+                issued[0] += 1
+        quantise_and_multiply(UNITS - 1)

@@ -32,8 +32,9 @@ UNITS = PAIRS * HALVES * 2
 CHUNKS_AHEAD = 6
 W_COLS = IMG + 1
 BANK_WINDOWS = 3
-SCALAR_GROUPS = (1, 2, 2, 2)
+SCALAR_GROUPS = (2, 2, 2, 2)
 IN_TWO_CALLS = (0, UNITS - 1)
+WARM_UP = 6
 
 
 def tile_conv2d_t_kernel(tc, x, weights, bias, grad_out, out):
@@ -124,10 +125,9 @@ def tile_conv2d_t_kernel(tc, x, weights, bias, grad_out, out):
                         out=target[:, b, 0:by_vector], in_=source[:, 4 * part : 4 * part + by_vector]
                     )
             else:
-                for g in range(by_vector, 4):
-                    for b in batches:
-                        source = loaded[(pair, half, b)][:].rearrange("p (t c g f) -> p g c t f", t=4, g=8, f=4)
-                        nc.scalar.copy(out=target[:, b, g], in_=source[:, 4 * part + g])
+                for b in batches:
+                    source = loaded[(pair, half, b)][:].rearrange("p (t c g f) -> p g c t f", t=4, g=8, f=4)
+                    nc.scalar.copy(out=target[:, b, by_vector:4], in_=source[:, 4 * part + by_vector : 4 * part + 4])
 
         def quantise_unit(unit):
             pair, rest = divmod(unit, 2 * HALVES)
@@ -234,15 +234,15 @@ def tile_conv2d_t_kernel(tc, x, weights, bias, grad_out, out):
         issued = [CHUNKS_AHEAD // 2]
 
         make_identity(nc, ident[:])
+        nc.gpsimd.tensor_copy(
+            out=sorter[:].rearrange("p (di j8 dj) -> p di j8 dj", di=KS, dj=KS),
+            in_=ident[:].rearrange("p (j8 di dj) -> p di j8 dj", di=KS, dj=KS),
+        )
         for pair in range(PAIRS + 1):
             col = IMG * pair * ROW
             end = (IMG * pair + PAD) * ROW if pair < PAIRS else IN_ROWS * ROW
             nc.vector.memset(g_words[:, :, col:end].bitcast(I32), 0)
             nc.vector.memset(g_scales[:, :, col:end].bitcast(I32), 0)
-        nc.vector.tensor_copy(
-            out=sorter[:].rearrange("p (di j8 dj) -> p di j8 dj", di=KS, dj=KS),
-            in_=ident[:].rearrange("p (j8 di dj) -> p di j8 dj", di=KS, dj=KS),
-        )
         nc.vector.memset(fold_f32[:], 0.0)
         for dj in range(KS):
             nc.vector.tensor_tensor(
@@ -253,6 +253,16 @@ def tile_conv2d_t_kernel(tc, x, weights, bias, grad_out, out):
             )
         nc.vector.tensor_copy(out=fold[:], in_=fold_f32[:])
         prepare_weights(0)
+        warm = result_banks.tile([P, WIN * ROW], F32, tag="result", name="warm")
+        for b in range(2):
+            for repeat in range(WARM_UP):
+                nc.tensor.matmul(
+                    out=warm[:],
+                    lhsT=loaded[(0, 0, b)][:, 0:P],
+                    rhs=loaded[(0, 0, b)][:, 0 : WIN * ROW],
+                    start=True,
+                    stop=True,
+                )
 
         def quantise_and_multiply(unit):
             quantise_unit(unit)

@@ -34,7 +34,7 @@ W_COLS = IMG + 1
 BANK_WINDOWS = 3
 SCALAR_GROUPS = (2, 2, 2, 2)
 IN_TWO_CALLS = (0, UNITS - 1)
-WARM_UP = 6
+WARM_UP = (6, 3)
 
 
 def tile_conv2d_t_kernel(tc, x, weights, bias, grad_out, out):
@@ -68,23 +68,32 @@ def tile_conv2d_t_kernel(tc, x, weights, bias, grad_out, out):
                 in_=weights.rearrange("(blk r) k -> r blk k", r=P)[:, :, half * K_PASS : (half + 1) * K_PASS],
             )
 
-        def prepare_weights(half):
+        turned = {}
+
+        def transpose_weights(half):
             words = w_rows[half][:].rearrange("p blk k -> p (blk k)").bitcast(F32)
-            w_pairs = w_grouped[:].bitcast(F32).rearrange(
-                "p (h di blk s e) -> p h blk di s e", h=HALVES, di=KS, blk=4, e=2
-            )
             for two in range(2):
-                turned = banks.tile([P, 4, P], F32, tag="bank", name="turned%d_%d" % (half, two))
+                turned[(half, two)] = banks.tile([P, 4, P], F32, tag="bank", name="turned%d_%d" % (half, two))
                 for blk in range(2):
                     for e in range(2):
                         word = (2 * two + blk) * (K_PASS // 2) + e
                         nc.tensor.transpose(
-                            turned[:, 2 * blk + e, :], words[:, word : word + K_PASS // 2 - 1 : 2], sorter[:]
+                            turned[(half, two)][:, 2 * blk + e, :],
+                            words[:, word : word + K_PASS // 2 - 1 : 2],
+                            sorter[:],
                         )
+
+        def quantise_weights(half):
+            w_pairs = w_grouped[:].bitcast(F32).rearrange(
+                "p (h di blk s e) -> p h blk di s e", h=HALVES, di=KS, blk=4, e=2
+            )
+            for two in range(2):
                 for blk in range(2):
                     nc.scalar.copy(
                         out=w_pairs[:, half, 2 * two + blk],
-                        in_=turned[:, 2 * blk : 2 * blk + 2, :].rearrange("p e (di s) -> p di s e", di=KS),
+                        in_=turned[(half, two)][:, 2 * blk : 2 * blk + 2, :].rearrange(
+                            "p e (di s) -> p di s e", di=KS
+                        ),
                     )
             cols = slice(half * K_PASS, (half + 1) * K_PASS)
             nc.vector.quantize_mx(
@@ -252,10 +261,11 @@ def tile_conv2d_t_kernel(tc, x, weights, bias, grad_out, out):
                 op=mybir.AluOpType.add,
             )
         nc.vector.tensor_copy(out=fold[:], in_=fold_f32[:])
-        prepare_weights(0)
+        transpose_weights(0)
+        quantise_weights(0)
         warm = result_banks.tile([P, WIN * ROW], F32, tag="result", name="warm")
         for b in range(2):
-            for repeat in range(WARM_UP):
+            for repeat in range(WARM_UP[b]):
                 nc.tensor.matmul(
                     out=warm[:],
                     lhsT=loaded[(0, 0, b)][:, 0:P],
@@ -263,11 +273,12 @@ def tile_conv2d_t_kernel(tc, x, weights, bias, grad_out, out):
                     start=True,
                     stop=True,
                 )
+        transpose_weights(1)
 
         def quantise_and_multiply(unit):
             quantise_unit(unit)
             if unit == 1:
-                prepare_weights(1)
+                quantise_weights(1)
             multiply(unit, issued[0] == len(load_order))
 
         for unit in range(UNITS):

@@ -27,13 +27,14 @@ WIN = 8
 OUT_ROWS = PAIRS * IMG
 WINDOWS = (OUT_ROWS + WIN - 1) // WIN
 IN_ROWS = WINDOWS * WIN + PAD
+FRONT = WINDOWS * WIN - OUT_ROWS
 UNIT = 16
 UNITS = PAIRS * HALVES * 2
 CHUNKS_AHEAD = 6
 W_COLS = IMG + 1
 BANK_WINDOWS = 3
 SCALAR_GROUPS = (2, 2, 2, 2)
-IN_TWO_CALLS = (0, UNITS - 1)
+CALL_ROWS = {0: (8, 8), UNITS - 1: (8, 4, 4)}
 WARM_UP = (6, 3)
 
 
@@ -126,7 +127,7 @@ def tile_conv2d_t_kernel(tc, x, weights, bias, grad_out, out):
                     [P, UNIT * ROW * 4], BF16, tag="grouped", align_bytes=64, name="grouped%d" % unit
                 )
             target = regrouped[unit][:].rearrange("p (g f b c t) -> p b g c t f", g=4, f=4, b=2, t=4)
-            by_vector = 2 if unit in IN_TWO_CALLS else 4 - SCALAR_GROUPS[rest]
+            by_vector = 2 if unit in CALL_ROWS else 4 - SCALAR_GROUPS[rest]
             if engine == "vector":
                 for b in batches:
                     source = loaded[(pair, half, b)][:].rearrange("p (t c g f) -> p g c t f", t=4, g=8, f=4)
@@ -134,22 +135,27 @@ def tile_conv2d_t_kernel(tc, x, weights, bias, grad_out, out):
                         out=target[:, b, 0:by_vector], in_=source[:, 4 * part : 4 * part + by_vector]
                     )
             else:
-                for b in batches:
-                    source = loaded[(pair, half, b)][:].rearrange("p (t c g f) -> p g c t f", t=4, g=8, f=4)
-                    nc.scalar.copy(out=target[:, b, by_vector:4], in_=source[:, 4 * part + by_vector : 4 * part + 4])
+                step = 1 if unit in CALL_ROWS else 4 - by_vector
+                for g in range(by_vector, 4, step):
+                    for b in batches:
+                        source = loaded[(pair, half, b)][:].rearrange("p (t c g f) -> p g c t f", t=4, g=8, f=4)
+                        nc.scalar.copy(
+                            out=target[:, b, g : g + step], in_=source[:, 4 * part + g : 4 * part + g + step]
+                        )
 
         def quantise_unit(unit):
             pair, rest = divmod(unit, 2 * HALVES)
             half, part = divmod(rest, 2)
-            calls = 2 if unit in IN_TWO_CALLS else 1
-            width = UNIT * ROW // calls
-            for call in range(calls):
-                col = (IMG * pair + PAD + UNIT * part) * ROW + call * width
+            first = 0
+            for rows in CALL_ROWS.get(unit, (UNIT,)):
+                col = (FRONT + IMG * pair + PAD + UNIT * part + first) * ROW
+                width = rows * ROW
                 nc.vector.quantize_mx(
                     out=g_words[:, half, col : col + width].bitcast(E5M2X4),
                     scales=g_scales[:, half, col : col + width],
-                    in_=regrouped[unit][:, 4 * call * width : 4 * (call + 1) * width],
+                    in_=regrouped[unit][:, 4 * first * ROW : 4 * (first + rows) * ROW],
                 )
+                first += rows
 
 
         sums = {}
@@ -163,8 +169,8 @@ def tile_conv2d_t_kernel(tc, x, weights, bias, grad_out, out):
             for window in finished[saved[0] :]:
                 for upper in range(2):
                     r = 0
-                    while r < 4 and WIN * window + 4 * upper + r < OUT_ROWS:
-                        pair, h = divmod(WIN * window + 4 * upper + r, IMG)
+                    while r < 4 and WIN * window + 4 * upper >= FRONT:
+                        pair, h = divmod(WIN * window + 4 * upper + r - FRONT, IMG)
                         n = min(4 - r, IMG - h)
                         nc.sync.dma_start(
                             out=out_rows[ROW * pair : ROW * (pair + 1), h * IMG : (h + n) * IMG],
@@ -206,11 +212,9 @@ def tile_conv2d_t_kernel(tc, x, weights, bias, grad_out, out):
             pair, rest = divmod(unit, 2 * HALVES)
             half, part = divmod(rest, 2)
             if part == 0:
-                rows_ready = IMG * pair + PAD + UNIT
-            elif pair < PAIRS - 1:
-                rows_ready = IMG * (pair + 1) + PAD
+                rows_ready = FRONT + IMG * pair + PAD + UNIT
             else:
-                rows_ready = IN_ROWS
+                rows_ready = FRONT + IMG * (pair + 1) + PAD
             while next_window[half] < WINDOWS and WIN * (next_window[half] + 1) + PAD <= rows_ready:
                 window = next_window[half]
                 next_window[half] += 1
@@ -248,8 +252,8 @@ def tile_conv2d_t_kernel(tc, x, weights, bias, grad_out, out):
             in_=ident[:].rearrange("p (j8 di dj) -> p di j8 dj", di=KS, dj=KS),
         )
         for pair in range(PAIRS + 1):
-            col = IMG * pair * ROW
-            end = (IMG * pair + PAD) * ROW if pair < PAIRS else IN_ROWS * ROW
+            col = (FRONT + IMG * pair) * ROW if pair > 0 else 0
+            end = (FRONT + IMG * pair + PAD) * ROW
             nc.vector.memset(g_words[:, :, col:end].bitcast(I32), 0)
             nc.vector.memset(g_scales[:, :, col:end].bitcast(I32), 0)
         nc.vector.memset(fold_f32[:], 0.0)

@@ -203,8 +203,14 @@ def tile_conv2d_t_kernel(tc, x, weights, bias, grad_out, out):
                         start=(term is hi),
                         stop=(term is lo),
                     )
-            nc.scalar.copy(out=results[:, window, :, :], in_=result_bank[0][:, place, :, 0:IMG])
-            finished.append(window)
+            if window >= WINDOWS - BANK_WINDOWS:
+                nc.scalar.copy(out=results[:, window, :, :], in_=result_bank[0][:, place, :, 0:IMG])
+                finished.append(window)
+            elif place == BANK_WINDOWS - 1:
+                nc.scalar.copy(
+                    out=results[:, window - place : window + 1, :, :], in_=result_bank[0][:, :, :, 0:IMG]
+                )
+                finished.extend(range(window - place, window + 1))
             if all_loads_issued:
                 save_results()
 

@@ -147,7 +147,7 @@ def tile_conv2d_t_kernel(tc, x, weights, bias, grad_out, out):
             pair, rest = divmod(unit, 2 * HALVES)
             half, part = divmod(rest, 2)
             first = 0
-            for rows in CALL_ROWS.get(unit, (UNIT,)):
+            for rows in CALL_ROWS.get(unit, (UNIT // 2, UNIT // 2)):
                 col = (FRONT + IMG * pair + PAD + UNIT * part + first) * ROW
                 width = rows * ROW
                 nc.vector.quantize_mx(

@@ -227,7 +227,7 @@ def tile_conv2d_t_kernel(tc, x, weights, bias, grad_out, out):
                 if window not in sums:
                     sums[window] = banks.tile([P, WIN * ROW], F32, tag="bank", name="sums%d" % window)
                     passes_done[window] = 0
-                for di in range(KS):
+                for di in reversed(range(KS)):
                     col = (WIN * window + PAD - di) * ROW
                     w_col = half * K_PASS + di * P
                     nc.tensor.matmul_mx(

@@ -292,8 +292,10 @@ def tile_conv2d_t_kernel(tc, x, weights, bias, grad_out, out):
             multiply(unit, issued[0] == len(load_order))
 
         for unit in range(UNITS):
+            if unit >= UNITS - 4:
+                quantise_and_multiply(unit - 1)
             regroup_unit(unit, "vector", (0,))
-            if unit > 0:
+            if 0 < unit < UNITS - 4:
                 quantise_and_multiply(unit - 1)
             regroup_unit(unit, "vector", (1,))
             regroup_unit(unit, "scalar", (0, 1))

from contextlib import ExitStack

import concourse.mybir as mybir
from concourse.masks import make_identity

FLOPS = 2 * 8192 * 1024 * 512
BYTES = 8 * 1024 * 1024 * 2 + 512 * 1024 * 2 + 8 * 32 * 35 * 35 * 4

BF16 = mybir.dt.bfloat16
F32 = mybir.dt.float32
I32 = mybir.dt.int32
U32 = mybir.dt.uint32
U8 = mybir.dt.uint8
E4M3X4 = mybir.dt.float8_e4m3fn_x4
E5M2X4 = mybir.dt.float8_e5m2_x4

P = 128
K_PASS = 512
HALVES = 2
KS = 4
TOKENS = 1024
IMG = 35
PAIRS = 4
ROW = 64
PAD = KS - 1
WIN = 8
OUT_ROWS = PAIRS * IMG
WINDOWS = (OUT_ROWS + WIN - 1) // WIN
IN_ROWS = WINDOWS * WIN + PAD
FRONT = WINDOWS * WIN - OUT_ROWS
UNIT = 16
UNITS = PAIRS * HALVES * 2
CHUNKS_AHEAD = 6
W_COLS = IMG + 1
BANK_WINDOWS = 3
SCALAR_GROUPS = (2, 2, 2, 2)
CALL_ROWS = {0: (8, 8), UNITS - 1: (8, 4, 4)}
WARM_UP = (6, 3)


def tile_conv2d_t_kernel(tc, x, weights, bias, grad_out, out):
    nc = tc.nc
    with ExitStack() as ctx:
        keep = ctx.enter_context(tc.tile_pool(name="keep", bufs=1))
        chunks = ctx.enter_context(tc.tile_pool(name="chunks", bufs=CHUNKS_AHEAD))
        work = ctx.enter_context(tc.tile_pool(name="work", bufs=4))
        banks = ctx.enter_context(tc.psum_pool(name="banks", bufs=6))
        result_banks = ctx.enter_context(tc.psum_pool(name="result_banks", bufs=2))

        g_words = keep.tile([P, HALVES, IN_ROWS * ROW], U32, align_bytes=64)
        g_scales = keep.tile([P, HALVES, IN_ROWS * ROW], U8, align_bytes=64)
        w_words = keep.tile([P, HALVES * K_PASS], U32, align_bytes=64)
        w_scales = keep.tile([P, HALVES * K_PASS], U8, align_bytes=64)
        w_rows_0 = keep.tile([P, 4, K_PASS], BF16)
        w_rows_1 = keep.tile([P, 4, K_PASS], BF16)
        w_rows = [w_rows_0, w_rows_1]
        w_grouped = keep.tile([P, HALVES * K_PASS * 4], BF16, align_bytes=64)
        ident = keep.tile([P, P], F32)
        sorter = keep.tile([P, P], F32)
        fold_f32 = keep.tile([P, W_COLS], F32)
        fold = keep.tile([P, W_COLS], BF16)
        results = keep.tile([P, WINDOWS, 4, IMG], F32)
        out_rows = out.rearrange("b c h w -> (b c) (h w)")


        def load_weights(half):
            nc.sync.dma_start(
                out=w_rows[half][:],
                in_=weights.rearrange("(blk r) k -> r blk k", r=P)[:, :, half * K_PASS : (half + 1) * K_PASS],
            )

        turned = {}

        def transpose_weights(half):
            words = w_rows[half][:].rearrange("p blk k -> p (blk k)").bitcast(F32)
            for two in range(2):
                turned[(half, two)] = banks.tile([P, 4, P], F32, tag="bank", name="turned%d_%d" % (half, two))
                for blk in range(2):
                    for e in range(2):
                        word = (2 * two + blk) * (K_PASS // 2) + e
                        nc.tensor.transpose(
                            turned[(half, two)][:, 2 * blk + e, :],
                            words[:, word : word + K_PASS // 2 - 1 : 2],
                            sorter[:],
                        )

        def quantise_weights(half):
            w_pairs = w_grouped[:].bitcast(F32).rearrange(
                "p (h di blk s e) -> p h blk di s e", h=HALVES, di=KS, blk=4, e=2
            )
            for two in range(2):
                for blk in range(2):
                    nc.scalar.copy(
                        out=w_pairs[:, half, 2 * two + blk],
                        in_=turned[(half, two)][:, 2 * blk : 2 * blk + 2, :].rearrange(
                            "p e (di s) -> p di s e", di=KS
                        ),
                    )
            cols = slice(half * K_PASS, (half + 1) * K_PASS)
            nc.vector.quantize_mx(
                out=w_words[:, cols].bitcast(E4M3X4),
                scales=w_scales[:, cols],
                in_=w_grouped[:, half * K_PASS * 4 : (half + 1) * K_PASS * 4],
            )


        loaded = {}

        def load_pair(pair, half):
            for b in range(2):
                chunk = chunks.tile([P, 4 * TOKENS], BF16, tag="chunk", name="chunk%d_%d_%d" % (pair, half, b))
                nc.sync.dma_start(
                    out=chunk[:],
                    in_=grad_out[2 * pair + b, half * K_PASS : (half + 1) * K_PASS].rearrange(
                        "(p t) c i -> p (t c i)", t=4
                    ),
                )
                loaded[(pair, half, b)] = chunk

        regrouped = {}

        def regroup_unit(unit, engine, batches):
            pair, rest = divmod(unit, 2 * HALVES)
            half, part = divmod(rest, 2)
            if unit not in regrouped:
                regrouped[unit] = work.tile(
                    [P, UNIT * ROW * 4], BF16, tag="grouped", align_bytes=64, name="grouped%d" % unit
                )
            target = regrouped[unit][:].rearrange("p (g f b c t) -> p b g c t f", g=4, f=4, b=2, t=4)
            by_vector = 2 if unit in CALL_ROWS else 4 - SCALAR_GROUPS[rest]
            if engine == "vector":
                for b in batches:
                    source = loaded[(pair, half, b)][:].rearrange("p (t c g f) -> p g c t f", t=4, g=8, f=4)
                    nc.vector.tensor_copy(
                        out=target[:, b, 0:by_vector], in_=source[:, 4 * part : 4 * part + by_vector]
                    )
            else:
                step = 1 if unit in CALL_ROWS else 4 - by_vector
                for g in range(by_vector, 4, step):
                    for b in batches:
                        source = loaded[(pair, half, b)][:].rearrange("p (t c g f) -> p g c t f", t=4, g=8, f=4)
                        nc.scalar.copy(
                            out=target[:, b, g : g + step], in_=source[:, 4 * part + g : 4 * part + g + step]
                        )

        def quantise_unit(unit):
            pair, rest = divmod(unit, 2 * HALVES)
            half, part = divmod(rest, 2)
            first = 0
            for rows in CALL_ROWS.get(unit, (UNIT // 2, UNIT // 2)):
                col = (FRONT + IMG * pair + PAD + UNIT * part + first) * ROW
                width = rows * ROW
                nc.vector.quantize_mx(
                    out=g_words[:, half, col : col + width].bitcast(E5M2X4),
                    scales=g_scales[:, half, col : col + width],
                    in_=regrouped[unit][:, 4 * first * ROW : 4 * (first + rows) * ROW],
                )
                first += rows


        sums = {}
        passes_done = {}
        next_window = [0, 0]
        result_bank = {}
        finished = []
        saved = [0]

        def save_results():
            for window in finished[saved[0] :]:
                for upper in range(2):
                    r = 0
                    while r < 4 and WIN * window + 4 * upper >= FRONT:
                        pair, h = divmod(WIN * window + 4 * upper + r - FRONT, IMG)
                        n = min(4 - r, IMG - h)
                        nc.sync.dma_start(
                            out=out_rows[ROW * pair : ROW * (pair + 1), h * IMG : (h + n) * IMG],
                            in_=results[ROW * upper : ROW * (upper + 1), window, r : r + n, :].rearrange(
                                "p r w -> p (r w)"
                            ),
                        )
                        r += n
            saved[0] = len(finished)

        def finish_window(window, all_loads_issued):
            bank = sums[window][:].rearrange("p (upper r col) -> p upper r col", upper=2, col=ROW)
            hi = work.tile([P, WIN * ROW], BF16, tag="hi", name="hi%d" % window)
            lo = work.tile([P, WIN * ROW], BF16, tag="lo", name="lo%d" % window)
            hi_rows = hi[:].rearrange("p (r upper col) -> p upper r col", upper=2, col=ROW)
            lo_rows = lo[:].rearrange("p (r upper col) -> p upper r col", upper=2, col=ROW)
            nc.scalar.copy(out=hi_rows, in_=bank)
            nc.vector.tensor_tensor(out=lo_rows, in0=bank, in1=hi_rows, op=mybir.AluOpType.subtract)
            place = window % BANK_WINDOWS
            if place == 0:
                result_bank[0] = result_banks.tile(
                    [P, BANK_WINDOWS, 4, W_COLS], F32, tag="result", name="result%d" % window
                )
            for r in range(4):
                for term in (hi, lo):
                    nc.tensor.matmul(
                        out=result_bank[0][:, place, r, :],
                        lhsT=term[:, r * P : (r + 1) * P],
                        rhs=fold[:],
                        start=(term is hi),
                        stop=(term is lo),
                    )
            if window >= WINDOWS - BANK_WINDOWS:
                nc.scalar.copy(out=results[:, window, :, :], in_=result_bank[0][:, place, :, 0:IMG])
                finished.append(window)
            elif place == BANK_WINDOWS - 1:
                nc.scalar.copy(
                    out=results[:, window - place : window + 1, :, :], in_=result_bank[0][:, :, :, 0:IMG]
                )
                finished.extend(range(window - place, window + 1))
            if all_loads_issued:
                save_results()

        def multiply(unit, all_loads_issued):
            pair, rest = divmod(unit, 2 * HALVES)
            half, part = divmod(rest, 2)
            if part == 0:
                rows_ready = FRONT + IMG * pair + PAD + UNIT
            else:
                rows_ready = FRONT + IMG * (pair + 1) + PAD
            while next_window[half] < WINDOWS and WIN * (next_window[half] + 1) + PAD <= rows_ready:
                window = next_window[half]
                next_window[half] += 1
                if window not in sums:
                    sums[window] = banks.tile([P, WIN * ROW], F32, tag="bank", name="sums%d" % window)
                    passes_done[window] = 0
                for di in reversed(range(KS)):
                    col = (WIN * window + PAD - di) * ROW
                    w_col = half * K_PASS + di * P
                    nc.tensor.matmul_mx(
                        out=sums[window][:],
                        lhsT=w_words[:, w_col : w_col + P].bitcast(E4M3X4),
                        lhsT_scale=w_scales[:, w_col : w_col + P],
                        rhs=g_words[:, half, col : col + WIN * ROW].bitcast(E5M2X4),
                        rhs_scale=g_scales[:, half, col : col + WIN * ROW],
                        start=(passes_done[window] == 0),
                        stop=(passes_done[window] == HALVES * KS - 1),
                    )
                    passes_done[window] += 1
                if passes_done[window] == HALVES * KS:
                    finish_window(window, all_loads_issued)


        load_order = [(pair, half) for pair in range(PAIRS) for half in range(HALVES)]
        load_weights(0)
        load_pair(*load_order[0])
        load_weights(1)
        load_pair(*load_order[1])
        load_pair(*load_order[2])
        issued = [CHUNKS_AHEAD // 2]

        make_identity(nc, ident[:])
        nc.gpsimd.tensor_copy(
            out=sorter[:].rearrange("p (di j8 dj) -> p di j8 dj", di=KS, dj=KS),
            in_=ident[:].rearrange("p (j8 di dj) -> p di j8 dj", di=KS, dj=KS),
        )
        for pair in range(PAIRS + 1):
            col = (FRONT + IMG * pair) * ROW if pair > 0 else 0
            end = (FRONT + IMG * pair + PAD) * ROW
            nc.vector.memset(g_words[:, :, col:end].bitcast(I32), 0)
            nc.vector.memset(g_scales[:, :, col:end].bitcast(I32), 0)
        nc.vector.memset(fold_f32[:], 0.0)
        for dj in range(KS):
            nc.vector.tensor_tensor(
                out=fold_f32[:, dj : dj + 32],
                in0=fold_f32[:, dj : dj + 32],
                in1=ident[:, dj:P:KS],
                op=mybir.AluOpType.add,
            )
        nc.vector.tensor_copy(out=fold[:], in_=fold_f32[:])
        transpose_weights(0)
        quantise_weights(0)
        warm = result_banks.tile([P, WIN * ROW], F32, tag="result", name="warm")
        for b in range(2):
            for repeat in range(WARM_UP[b]):
                nc.tensor.matmul(
                    out=warm[:],
                    lhsT=loaded[(0, 0, b)][:, 0:P],
                    rhs=loaded[(0, 0, b)][:, 0 : WIN * ROW],
                    start=True,
                    stop=True,
                )
        transpose_weights(1)

        def quantise_and_multiply(unit):
            quantise_unit(unit)
            if unit == 1:
                quantise_weights(1)
            multiply(unit, issued[0] == len(load_order))

        for unit in range(UNITS):
            if unit >= UNITS - 4:
                quantise_and_multiply(unit - 1)
            regroup_unit(unit, "vector", (0,))
            if 0 < unit < UNITS - 4:
                quantise_and_multiply(unit - 1)
            regroup_unit(unit, "vector", (1,))
            regroup_unit(unit, "scalar", (0, 1))
            if unit % 2 == 1 and issued[0] < len(load_order):
                load_pair(*load_order[issued[0]])
                issued[0] += 1
        quantise_and_multiply(UNITS - 1)
